import numpy as np
import ml_dtypes


def mxq(x, axis, fmt="e4m3"):
    dtype, down = {"e4m3": (ml_dtypes.float8_e4m3fn, 7), "e5m2": (ml_dtypes.float8_e5m2, 14)}[fmt]
    v = np.moveaxis(np.asarray(x, np.float32).astype(ml_dtypes.bfloat16).astype(np.float64), axis, -1)
    blocks = v.reshape(v.shape[:-1] + (-1, 32))
    amax = np.abs(blocks).max(-1, keepdims=True)
    byte = np.maximum(np.where(amax > 0, np.frexp(amax)[1] - 1 + 127, 0) - down, 1)
    scale = np.exp2(byte - 127.0)
    codes = (blocks / scale).astype(np.float32).astype(dtype).astype(np.float64)
    return np.moveaxis((codes * scale).reshape(v.shape), -1, axis)


WIDE = False


def mx_kscale(k):
    if not WIDE:
        return np.ones(k)
    levels = np.array([10, -10, 5, -5, 0])
    a = np.random.permutation(np.resize(levels, k // 512 * 4)).reshape(k // 512, 4)
    idx = np.arange(k)
    return np.exp2(a[idx // 512, idx % 128 // 32])


BF16 = ml_dtypes.bfloat16


def bf(x):
    return np.asarray(x, np.float32).astype(BF16)


def f64(x):
    return np.asarray(x).astype(np.float64)


B, K, M, D = 8192, 128, 4, 512
KM = K * M
SX = 1.2 / D ** 0.25
TINY = 1e-10


def softmax(v, axis):
    e = np.exp(v - v.max(axis, keepdims=True))
    return e / e.sum(axis, keepdims=True)


def setup_inputs():
    s = mx_kscale(D)
    return {"x": bf(np.random.standard_normal((B, D)) * SX * s),
            "gamma_class": bf(softmax(2.0 * np.random.standard_normal((B, K)), 1)),
            "mu": bf(np.random.standard_normal((K, M, D)) * SX * s),
            "cur_var": bf(np.random.uniform(0.8, 1.2, (K, M, D)) * s * s),
            "pi": bf((0.5 + np.random.random((K, M))) / M)}


def reference(x, gamma_class, mu, cur_var, pi):
    x = f64(x)
    mu = f64(mu).reshape(KM, D)
    cur_var = f64(cur_var).reshape(KM, D)
    inv_var = 1.0 / cur_var
    maha = ((mxq(x * x, 1, "e4m3") @ mxq(inv_var, 1, "e4m3").T)
            - 2.0 * (mxq(x, 1, "e4m3") @ mxq(mu * inv_var, 1, "e4m3").T)
            + np.sum(mu * mu * inv_var, axis=-1)[None])
    log_det = np.sum(np.log(cur_var), axis=-1)
    log_lik = -0.5 * (log_det[None] + maha)
    log_joint = (np.log(f64(pi) + TINY).reshape(KM)[None] + log_lik).reshape(B, K, M)
    top = log_joint.max(2, keepdims=True)
    lse = top + np.log(np.exp(log_joint - top).sum(2, keepdims=True))
    log_r = log_joint - lse
    return f64(gamma_class)[:, :, None] * np.exp(log_r)

@@ -1,0 +1,195 @@
+from contextlib import ExitStack
+
+import concourse.mybir as mybir
+from concourse.masks import make_identity
+
+F32 = mybir.dt.float32
+BF16 = mybir.dt.bfloat16
+U32 = mybir.dt.uint32
+U8 = mybir.dt.uint8
+FP8X4 = mybir.dt.float8_e4m3fn_x4
+ALU = mybir.AluOpType
+ACT = mybir.ActivationFunctionType
+AX = mybir.AxisListType
+
+P = 128
+B = 8192
+K = 128
+M = 4
+D = 512
+JT = B // P
+JB = 4
+NB = JT // JB
+W = JB * P
+FLOPS = 2 * 2 * B * K * M * D
+
+
+def tile_dota_mix_pa_t_kernel(tc, x, gamma_class, mu, cur_var, pi, out):
+    nc = tc.nc
+    xv = x.rearrange("(p j) d -> p j d", j=JT)
+    gv = gamma_class.rearrange("(p j) k -> p j k", j=JT)
+    ov = out.rearrange("(p j) k m -> p j (k m)", j=JT)
+
+    with ExitStack() as ctx:
+        const = ctx.enter_context(tc.tile_pool(name="const", bufs=1))
+        prep = ctx.enter_context(tc.tile_pool(name="prep", bufs=1))
+        xin = ctx.enter_context(tc.tile_pool(name="xin", bufs=3))
+        work = ctx.enter_context(tc.tile_pool(name="work", bufs=2))
+        big = ctx.enter_context(tc.tile_pool(name="big", bufs=3))
+        psum = ctx.enter_context(tc.psum_pool(name="psum", bufs=1))
+
+        var_sb = prep.tile([P, M, D], BF16)
+        nc.sync.dma_start(out=var_sb[:], in_=cur_var)
+        mu_sb = prep.tile([P, M, D], BF16)
+        nc.sync.dma_start(out=mu_sb[:], in_=mu)
+        pi_sb = prep.tile([P, M], BF16)
+        nc.scalar.dma_start(out=pi_sb[:], in_=pi)
+        g_sb = const.tile([P, JT, K], BF16)
+
+        identf = const.tile([P, P], F32)
+        make_identity(nc, identf[:])
+        identb = const.tile([P, P], BF16)
+        make_identity(nc, identb[:])
+
+        lnv = prep.tile([P, M, D], F32)
+        ld = prep.tile([P, M], F32)
+        for m in range(M):
+            nc.scalar.activation(out=lnv[:, m, :], in_=var_sb[:, m, :], func=ACT.Ln, accum_out=ld[:, m : m + 1])
+        pif = prep.tile([P, M], F32)
+        nc.vector.tensor_scalar_add(out=pif[:], in0=pi_sb[:], scalar1=1e-10)
+        lnpi = prep.tile([P, M], F32)
+        nc.scalar.activation(out=lnpi[:], in_=pif[:], func=ACT.Ln)
+
+        niv = prep.tile([P, M, D], F32)
+        nmiv = prep.tile([P, M, D], F32)
+        tmp = prep.tile([P, M, D], F32)
+        w1p = prep.tile([P, M, 4, P], BF16)
+        w2p = prep.tile([P, M, 4, P], BF16)
+        wg = prep.tile([P, 2, M, K * 4], BF16, align_bytes=64)
+        wq = const.tile([P, 2, M, K], U32, align_bytes=64)
+        ws = const.tile([P, 2, M, K], U8, align_bytes=64)
+        for m in range(M):
+            nc.scalar.activation(out=lnv[:, m, :], in_=lnv[:, m, :], func=ACT.Exp, scale=-1.0)
+            nc.vector.tensor_tensor(out=niv[:, m, :], in0=var_sb[:, m, :], in1=lnv[:, m, :], op=ALU.mult)
+            nc.vector.scalar_tensor_tensor(
+                out=niv[:, m, :], in0=niv[:, m, :], scalar=2.0, in1=lnv[:, m, :], op0=ALU.subtract, op1=ALU.mult
+            )
+            nc.vector.tensor_tensor(out=nmiv[:, m, :], in0=mu_sb[:, m, :], in1=niv[:, m, :], op=ALU.mult)
+            nc.scalar.activation(
+                out=w1p[:, m, :, :].rearrange("k (u e) q -> k u e q", e=2),
+                in_=niv[:, m, :].rearrange("k (u q e) -> k u e q", u=2, e=2),
+                func=ACT.Copy,
+                scale=0.5,
+            )
+            nc.scalar.activation(
+                out=w2p[:, m, :, :].rearrange("k (u e) q -> k u e q", e=2),
+                in_=nmiv[:, m, :].rearrange("k (u q e) -> k u e q", u=2, e=2),
+                func=ACT.Copy,
+                scale=-1.0,
+            )
+            nc.gpsimd.tensor_tensor(out=tmp[:, m, :], in0=nmiv[:, m, :], in1=mu_sb[:, m, :], op=ALU.mult)
+            for w, wp in enumerate((w1p, w2p)):
+                wt = psum.tile([P, 4, K], BF16, tag="et%d" % w, name="wt")
+                for t in range(4):
+                    nc.tensor.transpose(wt[:, t, :], wp[:, m, t, :], identb[:])
+                nc.vector.tensor_copy(
+                    out=wg[:, w, m, :].rearrange("p (k t) -> p k t", t=4), in_=wt[:].rearrange("p t k -> p k t")
+                )
+                nc.vector.quantize_mx(out=wq[:, w, m, :].bitcast(FP8X4), scales=ws[:, w, m, :], in_=wg[:, w, m, :])
+        qs = prep.tile([P, M], F32)
+        nc.vector.tensor_reduce(out=qs[:], in_=tmp[:], axis=AX.X, op=ALU.add)
+        nc.vector.tensor_tensor(out=qs[:], in0=qs[:], in1=ld[:], op=ALU.subtract)
+        bias = const.tile([P, M], F32)
+        nc.vector.scalar_tensor_tensor(out=bias[:], in0=qs[:], scalar=0.5, in1=lnpi[:], op0=ALU.mult, op1=ALU.add)
+
+        for i in range(NB):
+            js = slice(i * JB, (i + 1) * JB)
+            x_sb = xin.tile([P, JB, D], BF16)
+            nc.sync.dma_start(out=x_sb[:], in_=xv[:, js, :])
+            if i % 4 == 0:
+                nc.sync.dma_start(out=g_sb[:, i * JB : (i + 4) * JB, :], in_=gv[:, i * JB : (i + 4) * JB, :])
+            xw = x_sb[:].bitcast(F32)
+            xg = work.tile([P, W, 4], BF16, align_bytes=64)
+            x2g = work.tile([P, W, 4], BF16, align_bytes=64)
+            xgf = xg[:].bitcast(F32)
+            for half in range(2):
+                xt = psum.tile([P, 2, 2 * P], F32, tag="xt", name="xt")
+                for jj in range(2):
+                    for u in range(2):
+                        nc.tensor.transpose(
+                            xt[:, u, jj * P : (jj + 1) * P], xw[:, 2 * half + jj, u * P : (u + 1) * P], identf[:]
+                        )
+                cs = slice(half * 2 * P, (half + 1) * 2 * P)
+                nc.scalar.copy(out=xgf[:, cs, :], in_=xt[:].rearrange("p u c -> p c u"))
+                nc.scalar.activation(
+                    out=x2g[:, cs, :].rearrange("p c (u e) -> p c u e", e=2),
+                    in_=xt[:].bitcast(BF16).rearrange("p u (c e) -> p c u e", e=2),
+                    func=ACT.Square,
+                )
+            xq = work.tile([P, W], U32, align_bytes=64)
+            xs = work.tile([P, W], U8, align_bytes=64)
+            x2q = work.tile([P, W], U32, align_bytes=64)
+            x2s = work.tile([P, W], U8, align_bytes=64)
+            nc.vector.quantize_mx(out=xq[:].bitcast(FP8X4), scales=xs[:], in_=xg[:].rearrange("p c t -> p (c t)"))
+            nc.vector.quantize_mx(out=x2q[:].bitcast(FP8X4), scales=x2s[:], in_=x2g[:].rearrange("p c t -> p (c t)"))
+
+            pm = []
+            for m in range(M):
+                acc = psum.tile([P, W], F32, tag="p%d" % m, name="acc")
+                nc.tensor.matmul_mx(
+                    out=acc[:],
+                    lhsT=wq[:, 0, m, :].bitcast(FP8X4),
+                    lhsT_scale=ws[:, 0, m, :],
+                    rhs=x2q[:].bitcast(FP8X4),
+                    rhs_scale=x2s[:],
+                    start=True,
+                    stop=False,
+                )
+                nc.tensor.matmul_mx(
+                    out=acc[:],
+                    lhsT=wq[:, 1, m, :].bitcast(FP8X4),
+                    lhsT_scale=ws[:, 1, m, :],
+                    rhs=xq[:].bitcast(FP8X4),
+                    rhs_scale=xs[:],
+                    start=False,
+                    stop=True,
+                )
+                pm.append(acc)
+
+            top = work.tile([P, W], F32)
+            nc.scalar.activation(out=top[:], in_=pm[0][:], func=ACT.Identity, bias=bias[:, 0:1])
+            for m in range(1, M):
+                nc.vector.scalar_tensor_tensor(
+                    out=top[:], in0=pm[m][:], scalar=bias[:, m : m + 1], in1=top[:], op0=ALU.add, op1=ALU.max
+                )
+            de = big.tile([P, M, W], F32)
+            for m in range(M):
+                nc.vector.scalar_tensor_tensor(
+                    out=de[:, m, :], in0=pm[m][:], scalar=bias[:, m : m + 1], in1=top[:], op0=ALU.add, op1=ALU.subtract
+                )
+                nc.scalar.activation(out=de[:, m, :], in_=de[:, m, :], func=ACT.Exp)
+            hs = work.tile([P, 2, W], F32)
+            nc.gpsimd.tensor_tensor(out=hs[:], in0=de[:, 0:2, :], in1=de[:, 2:4, :], op=ALU.add)
+            ssum = work.tile([P, W], F32)
+            nc.gpsimd.tensor_tensor(out=ssum[:], in0=hs[:, 0, :], in1=hs[:, 1, :], op=ALU.add)
+
+            rt = psum.tile([P, JB, K], F32, tag="rt", name="rt")
+            for jl in range(JB):
+                nc.tensor.transpose(rt[:, jl, :], ssum[:, jl * P : (jl + 1) * P], identf[:])
+            rc = work.tile([P, JB, K], F32)
+            nc.vector.reciprocal(out=rc[:], in_=rt[:])
+            rr = work.tile([P, JB, K], F32)
+            nc.gpsimd.tensor_tensor(out=rr[:], in0=rc[:], in1=g_sb[:, js, :], op=ALU.mult)
+
+            o_sb = big.tile([P, JB, K * M], F32)
+            for jl in range(JB):
+                et = psum.tile([P, M, K], F32, tag="et%d" % (jl % 2), name="et")
+                for m in range(M):
+                    nc.tensor.transpose(et[:, m, :], de[:, m, jl * P : (jl + 1) * P], identf[:])
+                nc.vector.tensor_tensor(
+                    out=o_sb[:, jl, :].rearrange("p (k m) -> p k m", m=M),
+                    in0=et[:].rearrange("p m k -> p k m"),
+                    in1=rr[:, jl, :].unsqueeze(2).to_broadcast([P, K, M]),
+                    op=ALU.mult,
+                )
+            nc.sync.dma_start(out=ov[:, js, :], in_=o_sb[:])

@@ -10,7 +10,6 @@ U8 = mybir.dt.uint8
 FP8X4 = mybir.dt.float8_e4m3fn_x4
 ALU = mybir.AluOpType
 ACT = mybir.ActivationFunctionType
-AX = mybir.AxisListType
 
 P = 128
 B = 8192
@@ -23,6 +22,11 @@ NB = JT // JB
 W = JB * P
 FLOPS = 2 * 2 * B * K * M * D
 
+XL = 3
+GROUPS = ((0, 3), (4, 7), (8, 11), (12, 13), (14, 14), (15, 15))
+LAGX = 4
+SQ_ON_G = True
+
 
 def tile_dota_mix_pa_t_kernel(tc, x, gamma_class, mu, cur_var, pi, out):
     nc = tc.nc
@@ -30,166 +34,340 @@ def tile_dota_mix_pa_t_kernel(tc, x, gamma_class, mu, cur_var, pi, out):
     gv = gamma_class.rearrange("(p j) k -> p j k", j=JT)
     ov = out.rearrange("(p j) k m -> p j (k m)", j=JT)
 
+    fn_at = {}
+    ln_at = {}
+    prev = -1
+    for a, b in GROUPS:
+        ln_at[b + 2] = (a, b)
+        for i in range(a, b + 1):
+            prev = max(prev + 1, b + LAGX)
+            fn_at[prev] = i
+    last_step = prev
+
     with ExitStack() as ctx:
+        ctx.enter_context(tc.manual_schedule())
         const = ctx.enter_context(tc.tile_pool(name="const", bufs=1))
-        prep = ctx.enter_context(tc.tile_pool(name="prep", bufs=1))
-        xin = ctx.enter_context(tc.tile_pool(name="xin", bufs=3))
-        work = ctx.enter_context(tc.tile_pool(name="work", bufs=2))
-        big = ctx.enter_context(tc.tile_pool(name="big", bufs=3))
+        xin = ctx.enter_context(tc.tile_pool(name="xin", bufs=4))
+        grp = ctx.enter_context(tc.tile_pool(name="grp", bufs=3))
+        cod = ctx.enter_context(tc.tile_pool(name="cod", bufs=3))
+        two = ctx.enter_context(tc.tile_pool(name="two", bufs=2))
+        tops = ctx.enter_context(tc.tile_pool(name="tops", bufs=4))
+        sums = ctx.enter_context(tc.tile_pool(name="sums", bufs=8))
+        outp = ctx.enter_context(tc.tile_pool(name="outp", bufs=3))
         psum = ctx.enter_context(tc.psum_pool(name="psum", bufs=1))
 
-        var_sb = prep.tile([P, M, D], BF16)
-        nc.sync.dma_start(out=var_sb[:], in_=cur_var)
-        mu_sb = prep.tile([P, M, D], BF16)
-        nc.sync.dma_start(out=mu_sb[:], in_=mu)
-        pi_sb = prep.tile([P, M], BF16)
-        nc.scalar.dma_start(out=pi_sb[:], in_=pi)
-        g_sb = const.tile([P, JT, K], BF16)
+        identf = const.tile([P, P], F32, name="identf")
+        identb = const.tile([P, P], BF16, name="identb")
+        wq = const.tile([P, 2, M, K], U32, name="wq", align_bytes=64)
+        ws = const.tile([P, 2, M, K], U8, name="ws", align_bytes=64)
+        bd = const.tile([P, M], F32, name="bd")
+        g_sb = const.tile([P, JT, K], BF16, name="g_sb")
 
-        identf = const.tile([P, P], F32)
-        make_identity(nc, identf[:])
-        identb = const.tile([P, P], BF16)
-        make_identity(nc, identb[:])
+        x_t = {}
+        xt_t = {}
+        xg_t = {}
+        x2g_t = {}
+        q_t = {}
+        pd_t = {}
+        top_t = {}
+        de_t = {}
+        s_t = {}
+        rt_t = {}
+        rr_t = {}
+        et_t = {}
+        o_t = {}
+        pools = {}
 
-        lnv = prep.tile([P, M, D], F32)
-        ld = prep.tile([P, M], F32)
-        for m in range(M):
-            nc.scalar.activation(out=lnv[:, m, :], in_=var_sb[:, m, :], func=ACT.Ln, accum_out=ld[:, m : m + 1])
-        pif = prep.tile([P, M], F32)
-        nc.vector.tensor_scalar_add(out=pif[:], in0=pi_sb[:], scalar1=1e-10)
-        lnpi = prep.tile([P, M], F32)
-        nc.scalar.activation(out=lnpi[:], in_=pif[:], func=ACT.Ln)
+        def load_x(i):
+            x_t[i] = xin.tile([P, JB, D], BF16, name="x_sb")
+            nc.sync.dma_start(out=x_t[i][:], in_=xv[:, i * JB : (i + 1) * JB, :])
 
-        niv = prep.tile([P, M, D], F32)
-        nmiv = prep.tile([P, M, D], F32)
-        tmp = prep.tile([P, M, D], F32)
-        w1p = prep.tile([P, M, 4, P], BF16)
-        w2p = prep.tile([P, M, 4, P], BF16)
-        wg = prep.tile([P, 2, M, K * 4], BF16, align_bytes=64)
-        wq = const.tile([P, 2, M, K], U32, align_bytes=64)
-        ws = const.tile([P, 2, M, K], U8, align_bytes=64)
-        for m in range(M):
-            nc.scalar.activation(out=lnv[:, m, :], in_=lnv[:, m, :], func=ACT.Exp, scale=-1.0)
-            nc.vector.tensor_tensor(out=niv[:, m, :], in0=var_sb[:, m, :], in1=lnv[:, m, :], op=ALU.mult)
+        def load_g(c):
+            nc.sync.dma_start(out=g_sb[:, c * 16 : (c + 1) * 16, :], in_=gv[:, c * 16 : (c + 1) * 16, :])
+
+        def xpose(i, h):
+            xt = psum.tile([P, 2, 2 * P], F32, tag="xt%d" % h, name="xt")
+            xw = x_t[i][:].bitcast(F32)
+            for jj in range(2):
+                for u in range(2):
+                    nc.tensor.transpose(xt[:, u, jj * P : (jj + 1) * P], xw[:, 2 * h + jj, u * P : (u + 1) * P], identf[:])
+            xt_t[(i, h)] = xt
+
+        def words(i, h, on_vector):
+            if h == 0:
+                xg_t[i] = grp.tile([P, W, 4], BF16, name="xg", align_bytes=64)
+                x2g_t[i] = grp.tile([P, W, 4], BF16, name="x2g", align_bytes=64)
+            cs = slice(h * 2 * P, (h + 1) * 2 * P)
+            dst = xg_t[i][:].bitcast(F32)[:, cs, :]
+            src = xt_t[(i, h)][:].rearrange("p u c -> p c u")
+            if on_vector:
+                nc.vector.tensor_copy(out=dst, in_=src)
+            else:
+                nc.scalar.copy(out=dst, in_=src)
+
+        def square_s(i, h):
+            cs = slice(h * 2 * P, (h + 1) * 2 * P)
+            nc.scalar.activation(
+                out=x2g_t[i][:, cs, :].rearrange("p c (u e) -> p c u e", e=2),
+                in_=xt_t[(i, h)][:].bitcast(BF16).rearrange("p u (c e) -> p c u e", e=2),
+                func=ACT.Square,
+            )
+
+        def square_sb(i, cs, eng):
+            a = xg_t[i][:, cs, :].rearrange("p c t -> p (c t)")
+            eng.tensor_tensor(out=x2g_t[i][:, cs, :].rearrange("p c t -> p (c t)"), in0=a, in1=a, op=ALU.mult)
+
+        def quant(i):
+            xq = cod.tile([P, W], U32, name="xq", align_bytes=64)
+            xs = cod.tile([P, W], U8, name="xs", align_bytes=64)
+            x2q = cod.tile([P, W], U32, name="x2q", align_bytes=64)
+            x2s = cod.tile([P, W], U8, name="x2s", align_bytes=64)
+            nc.vector.quantize_mx(out=xq[:].bitcast(FP8X4), scales=xs[:], in_=xg_t[i][:].rearrange("p c t -> p (c t)"))
+            nc.vector.quantize_mx(out=x2q[:].bitcast(FP8X4), scales=x2s[:], in_=x2g_t[i][:].rearrange("p c t -> p (c t)"))
+            q_t[i] = (x2q, x2s, xq, xs)
+
+        def mx(i, m):
+            acc = psum.tile([P, W], F32, tag="p%d" % m, name="acc")
+            passes = ((0, m), (0, 0), (1, m), (1, 0))
+            for n, (w, mm) in enumerate(passes):
+                nc.tensor.matmul_mx(
+                    out=acc[:],
+                    lhsT=wq[:, w, mm, :].bitcast(FP8X4),
+                    lhsT_scale=ws[:, w, mm, :],
+                    rhs=q_t[i][2 * w][:].bitcast(FP8X4),
+                    rhs_scale=q_t[i][2 * w + 1][:],
+                    start=(n == 0),
+                    stop=(n == 3),
+                )
+            pd_t[(i, m)] = acc
+
+        def chain(i):
+            top = tops.tile([P, W], F32, name="top")
+            top_t[i] = top
+            nc.vector.tensor_scalar(
+                out=top[:], in0=pd_t[(i, 1)][:], scalar1=bd[:, 1:2], scalar2=0.0, op0=ALU.add, op1=ALU.max
+            )
+            for m in (2, 3):
+                nc.vector.scalar_tensor_tensor(
+                    out=top[:], in0=pd_t[(i, m)][:], scalar=bd[:, m : m + 1], in1=top[:], op0=ALU.add, op1=ALU.max
+                )
+
+        def diff(i, m):
+            if m == 1:
+                de_t[i] = pools["big"].tile([P, M, W], F32, name="de")
             nc.vector.scalar_tensor_tensor(
-                out=niv[:, m, :], in0=niv[:, m, :], scalar=2.0, in1=lnv[:, m, :], op0=ALU.subtract, op1=ALU.mult
+                out=de_t[i][:, m, :],
+                in0=pd_t[(i, m)][:],
+                scalar=bd[:, m : m + 1],
+                in1=top_t[i][:],
+                op0=ALU.add,
+                op1=ALU.subtract,
             )
-            nc.vector.tensor_tensor(out=nmiv[:, m, :], in0=mu_sb[:, m, :], in1=niv[:, m, :], op=ALU.mult)
-            nc.scalar.activation(
-                out=w1p[:, m, :, :].rearrange("k (u e) q -> k u e q", e=2),
-                in_=niv[:, m, :].rearrange("k (u q e) -> k u e q", u=2, e=2),
-                func=ACT.Copy,
-                scale=0.5,
-            )
-            nc.scalar.activation(
-                out=w2p[:, m, :, :].rearrange("k (u e) q -> k u e q", e=2),
-                in_=nmiv[:, m, :].rearrange("k (u q e) -> k u e q", u=2, e=2),
-                func=ACT.Copy,
-                scale=-1.0,
-            )
-            nc.gpsimd.tensor_tensor(out=tmp[:, m, :], in0=nmiv[:, m, :], in1=mu_sb[:, m, :], op=ALU.mult)
-            for w, wp in enumerate((w1p, w2p)):
-                wt = psum.tile([P, 4, K], BF16, tag="et%d" % w, name="wt")
-                for t in range(4):
-                    nc.tensor.transpose(wt[:, t, :], wp[:, m, t, :], identb[:])
-                nc.vector.tensor_copy(
-                    out=wg[:, w, m, :].rearrange("p (k t) -> p k t", t=4), in_=wt[:].rearrange("p t k -> p k t")
-                )
-                nc.vector.quantize_mx(out=wq[:, w, m, :].bitcast(FP8X4), scales=ws[:, w, m, :], in_=wg[:, w, m, :])
-        qs = prep.tile([P, M], F32)
-        nc.vector.tensor_reduce(out=qs[:], in_=tmp[:], axis=AX.X, op=ALU.add)
-        nc.vector.tensor_tensor(out=qs[:], in0=qs[:], in1=ld[:], op=ALU.subtract)
-        bias = const.tile([P, M], F32)
-        nc.vector.scalar_tensor_tensor(out=bias[:], in0=qs[:], scalar=0.5, in1=lnpi[:], op0=ALU.mult, op1=ALU.add)
 
-        for i in range(NB):
-            js = slice(i * JB, (i + 1) * JB)
-            x_sb = xin.tile([P, JB, D], BF16)
-            nc.sync.dma_start(out=x_sb[:], in_=xv[:, js, :])
-            if i % 4 == 0:
-                nc.sync.dma_start(out=g_sb[:, i * JB : (i + 4) * JB, :], in_=gv[:, i * JB : (i + 4) * JB, :])
-            xw = x_sb[:].bitcast(F32)
-            xg = work.tile([P, W, 4], BF16, align_bytes=64)
-            x2g = work.tile([P, W, 4], BF16, align_bytes=64)
-            xgf = xg[:].bitcast(F32)
-            for half in range(2):
-                xt = psum.tile([P, 2, 2 * P], F32, tag="xt", name="xt")
-                for jj in range(2):
-                    for u in range(2):
-                        nc.tensor.transpose(
-                            xt[:, u, jj * P : (jj + 1) * P], xw[:, 2 * half + jj, u * P : (u + 1) * P], identf[:]
-                        )
-                cs = slice(half * 2 * P, (half + 1) * 2 * P)
-                nc.scalar.copy(out=xgf[:, cs, :], in_=xt[:].rearrange("p u c -> p c u"))
-                nc.scalar.activation(
-                    out=x2g[:, cs, :].rearrange("p c (u e) -> p c u e", e=2),
-                    in_=xt[:].bitcast(BF16).rearrange("p u (c e) -> p c u e", e=2),
-                    func=ACT.Square,
-                )
-            xq = work.tile([P, W], U32, align_bytes=64)
-            xs = work.tile([P, W], U8, align_bytes=64)
-            x2q = work.tile([P, W], U32, align_bytes=64)
-            x2s = work.tile([P, W], U8, align_bytes=64)
-            nc.vector.quantize_mx(out=xq[:].bitcast(FP8X4), scales=xs[:], in_=xg[:].rearrange("p c t -> p (c t)"))
-            nc.vector.quantize_mx(out=x2q[:].bitcast(FP8X4), scales=x2s[:], in_=x2g[:].rearrange("p c t -> p (c t)"))
+        def expo(i):
+            de = de_t[i]
+            nc.scalar.activation(out=de[:, 0, :], in_=top_t[i][:], func=ACT.Exp, scale=-1.0)
+            nc.scalar.activation(out=de[:, 1:4, :], in_=de[:, 1:4, :], func=ACT.Exp)
 
-            pm = []
-            for m in range(M):
-                acc = psum.tile([P, W], F32, tag="p%d" % m, name="acc")
-                nc.tensor.matmul_mx(
-                    out=acc[:],
-                    lhsT=wq[:, 0, m, :].bitcast(FP8X4),
-                    lhsT_scale=ws[:, 0, m, :],
-                    rhs=x2q[:].bitcast(FP8X4),
-                    rhs_scale=x2s[:],
-                    start=True,
-                    stop=False,
-                )
-                nc.tensor.matmul_mx(
-                    out=acc[:],
-                    lhsT=wq[:, 1, m, :].bitcast(FP8X4),
-                    lhsT_scale=ws[:, 1, m, :],
-                    rhs=xq[:].bitcast(FP8X4),
-                    rhs_scale=xs[:],
-                    start=False,
-                    stop=True,
-                )
-                pm.append(acc)
-
-            top = work.tile([P, W], F32)
-            nc.scalar.activation(out=top[:], in_=pm[0][:], func=ACT.Identity, bias=bias[:, 0:1])
-            for m in range(1, M):
-                nc.vector.scalar_tensor_tensor(
-                    out=top[:], in0=pm[m][:], scalar=bias[:, m : m + 1], in1=top[:], op0=ALU.add, op1=ALU.max
-                )
-            de = big.tile([P, M, W], F32)
-            for m in range(M):
-                nc.vector.scalar_tensor_tensor(
-                    out=de[:, m, :], in0=pm[m][:], scalar=bias[:, m : m + 1], in1=top[:], op0=ALU.add, op1=ALU.subtract
-                )
-                nc.scalar.activation(out=de[:, m, :], in_=de[:, m, :], func=ACT.Exp)
-            hs = work.tile([P, 2, W], F32)
+        def summ(i):
+            de = de_t[i]
+            hs = two.tile([P, 2, W], F32, name="hs")
             nc.gpsimd.tensor_tensor(out=hs[:], in0=de[:, 0:2, :], in1=de[:, 2:4, :], op=ALU.add)
-            ssum = work.tile([P, W], F32)
-            nc.gpsimd.tensor_tensor(out=ssum[:], in0=hs[:, 0, :], in1=hs[:, 1, :], op=ALU.add)
+            s_t[i] = sums.tile([P, W], F32, name="ssum")
+            nc.gpsimd.tensor_tensor(out=s_t[i][:], in0=hs[:, 0, :], in1=hs[:, 1, :], op=ALU.add)
 
+        def logs(i):
+            nc.scalar.activation(out=s_t[i][:], in_=s_t[i][:], func=ACT.Ln)
+
+        def recs(i):
+            nc.scalar.activation(out=s_t[i][:], in_=s_t[i][:], func=ACT.Exp, scale=-1.0)
+
+        def rpose(i):
             rt = psum.tile([P, JB, K], F32, tag="rt", name="rt")
             for jl in range(JB):
-                nc.tensor.transpose(rt[:, jl, :], ssum[:, jl * P : (jl + 1) * P], identf[:])
-            rc = work.tile([P, JB, K], F32)
-            nc.vector.reciprocal(out=rc[:], in_=rt[:])
-            rr = work.tile([P, JB, K], F32)
-            nc.gpsimd.tensor_tensor(out=rr[:], in0=rc[:], in1=g_sb[:, js, :], op=ALU.mult)
+                nc.tensor.transpose(rt[:, jl, :], s_t[i][:, jl * P : (jl + 1) * P], identf[:])
+            rt_t[i] = rt
 
-            o_sb = big.tile([P, JB, K * M], F32)
-            for jl in range(JB):
-                et = psum.tile([P, M, K], F32, tag="et%d" % (jl % 2), name="et")
-                for m in range(M):
-                    nc.tensor.transpose(et[:, m, :], de[:, m, jl * P : (jl + 1) * P], identf[:])
-                nc.vector.tensor_tensor(
-                    out=o_sb[:, jl, :].rearrange("p (k m) -> p k m", m=M),
-                    in0=et[:].rearrange("p m k -> p k m"),
-                    in1=rr[:, jl, :].unsqueeze(2).to_broadcast([P, K, M]),
-                    op=ALU.mult,
+        def gmul(i):
+            rr_t[i] = two.tile([P, JB, K], F32, name="rr")
+            nc.vector.tensor_tensor(out=rr_t[i][:], in0=rt_t[i][:], in1=g_sb[:, i * JB : (i + 1) * JB, :], op=ALU.mult)
+            o_t[i] = outp.tile([P, JB, K * M], F32, name="o_sb")
+
+        def epose(i, jl):
+            et = psum.tile([P, M, K], F32, tag="et%d" % (jl % 2), name="et")
+            for m in range(M):
+                nc.tensor.transpose(et[:, m, :], de_t[i][:, m, jl * P : (jl + 1) * P], identf[:])
+            et_t[(i, jl)] = et
+
+        def final(i, jl):
+            nc.vector.tensor_tensor(
+                out=o_t[i][:, jl, :].rearrange("p (k m) -> p k m", m=M),
+                in0=et_t[(i, jl)][:].rearrange("p m k -> p k m"),
+                in1=rr_t[i][:, jl, :].unsqueeze(2).to_broadcast([P, K, M]),
+                op=ALU.mult,
+            )
+
+        def store(i):
+            nc.sync.dma_start(out=ov[:, i * JB : (i + 1) * JB, :], in_=o_t[i][:])
+
+        with tc.tile_pool(name="prep", bufs=1) as prep:
+            var_sb = prep.tile([P, M, D], BF16, name="var_sb")
+            mu_sb = prep.tile([P, M, D], BF16, name="mu_sb")
+            pi_sb = prep.tile([P, M], BF16, name="pi_sb")
+            nc.sync.dma_start(out=var_sb[:], in_=cur_var)
+            load_x(0)
+            nc.sync.dma_start(out=mu_sb[:], in_=mu)
+            nc.scalar.dma_start(out=pi_sb[:], in_=pi)
+            load_x(1)
+            load_x(2)
+            load_x(3)
+            make_identity(nc, identf[:])
+            make_identity(nc, identb[:])
+
+            lnv = prep.tile([P, M, D], F32, name="lnv")
+            ld = prep.tile([P, M], F32, name="ld")
+            pif = prep.tile([P, M], F32, name="pif")
+            lnpi = prep.tile([P, M], F32, name="lnpi")
+            niv = prep.tile([P, M, D], F32, name="niv")
+            nmiv = prep.tile([P, M, D], F32, name="nmiv")
+            tmp = prep.tile([P, M, D], F32, name="tmp")
+            w1p = prep.tile([P, M, 4, P], BF16, name="w1p")
+            w2p = prep.tile([P, M, 4, P], BF16, name="w2p")
+            wg = prep.tile([P, 2, M, K * 4], BF16, name="wg", align_bytes=64)
+            qs = prep.tile([P, M], F32, name="qs")
+            bias = prep.tile([P, M], F32, name="bias")
+
+            for m in range(M):
+                nc.scalar.activation(out=lnv[:, m, :], in_=var_sb[:, m, :], func=ACT.Ln, accum_out=ld[:, m : m + 1])
+            nc.vector.tensor_scalar_add(out=pif[:], in0=pi_sb[:], scalar1=1e-10)
+            nc.scalar.activation(out=lnpi[:], in_=pif[:], func=ACT.Ln)
+
+            xpose(0, 0)
+            xpose(0, 1)
+            words(0, 0, True)
+            words(0, 1, True)
+            square_sb(0, slice(0, W), nc.vector)
+            quant(0)
+
+            for m in range(M):
+                nc.scalar.activation(out=lnv[:, m, :], in_=lnv[:, m, :], func=ACT.Exp, scale=-1.0)
+
+            def newton(m):
+                nc.vector.tensor_tensor(out=niv[:, m, :], in0=var_sb[:, m, :], in1=lnv[:, m, :], op=ALU.mult)
+                nc.vector.scalar_tensor_tensor(
+                    out=niv[:, m, :], in0=niv[:, m, :], scalar=2.0, in1=lnv[:, m, :], op0=ALU.subtract, op1=ALU.mult
                 )
-            nc.sync.dma_start(out=ov[:, js, :], in_=o_sb[:])
+                nc.vector.tensor_tensor(out=nmiv[:, m, :], in0=mu_sb[:, m, :], in1=niv[:, m, :], op=ALU.mult)
+
+            def casts(m):
+                sign = -1.0 if m == 0 else 1.0
+                nc.scalar.activation(
+                    out=w1p[:, m, :, :].rearrange("k (u e) q -> k u e q", e=2),
+                    in_=niv[:, m, :].rearrange("k (u q e) -> k u e q", u=2, e=2),
+                    func=ACT.Copy,
+                    scale=0.5 * sign,
+                )
+                nc.gpsimd.tensor_scalar(
+                    out=w2p[:, m, :, :].rearrange("k (u e) q -> k u e q", e=2),
+                    in0=nmiv[:, m, :].rearrange("k (u q e) -> k u e q", u=2, e=2),
+                    scalar1=-1.0 * sign,
+                    scalar2=0.0,
+                    op0=ALU.mult,
+                    op1=ALU.add,
+                )
+                nc.gpsimd.tensor_tensor(out=tmp[:, m, :], in0=nmiv[:, m, :], in1=mu_sb[:, m, :], op=ALU.mult)
+
+            def wpose(m):
+                for w, wp in enumerate((w1p, w2p)):
+                    wt = psum.tile([P, 4, K], BF16, tag="et%d" % w, name="wt")
+                    for t in range(4):
+                        nc.tensor.transpose(wt[:, t, :], wp[:, m, t, :], identb[:])
+                    nc.scalar.copy(out=wg[:, w, m, :].rearrange("p (k t) -> p k t", t=4), in_=wt[:].rearrange("p t k -> p k t"))
+
+            def wquant(m):
+                for w in range(2):
+                    nc.vector.quantize_mx(out=wq[:, w, m, :].bitcast(FP8X4), scales=ws[:, w, m, :], in_=wg[:, w, m, :])
+
+            newton(0)
+            casts(0)
+            newton(1)
+            casts(1)
+            wpose(0)
+            newton(2)
+            casts(2)
+            wpose(1)
+            wquant(0)
+            newton(3)
+            casts(3)
+            wpose(2)
+            wquant(1)
+            wpose(3)
+            wquant(2)
+            wquant(3)
+            for m in range(M):
+                nc.scalar.activation(out=tmp[:, m, :], in_=tmp[:, m, :], func=ACT.Copy, accum_out=qs[:, m : m + 1])
+            nc.vector.tensor_tensor(out=qs[:], in0=qs[:], in1=ld[:], op=ALU.subtract)
+            nc.vector.scalar_tensor_tensor(out=bias[:], in0=qs[:], scalar=0.5, in1=lnpi[:], op0=ALU.mult, op1=ALU.add)
+            nc.vector.tensor_scalar(out=bd[:], in0=bias[:], scalar1=bias[:, 0:1], scalar2=None, op0=ALU.subtract)
+
+        pools["big"] = ctx.enter_context(tc.tile_pool(name="big", bufs=8))
+
+        for t in range(-2, last_step + 1):
+            f = fn_at.get(t, -1)
+            nx = t + XL
+            if XL + 1 <= nx + 1 < NB:
+                load_x(nx + 1)
+            if 0 <= t < 4:
+                load_g(t)
+            if f >= 0:
+                rpose(f)
+                epose(f, 0)
+                epose(f, 1)
+            if 1 <= nx < NB:
+                xpose(nx, 0)
+                xpose(nx, 1)
+            grp_now = ln_at.get(t, None)
+            if grp_now is not None:
+                for i in range(grp_now[0], grp_now[1] + 1):
+                    logs(i)
+            elif 0 <= t - 1 < NB:
+                expo(t - 1)
+            if 1 <= nx < NB:
+                words(nx, 0, False)
+                square_s(nx, 0)
+                words(nx, 1, False)
+                if SQ_ON_G:
+                    square_sb(nx, slice(2 * P, W), nc.gpsimd)
+                else:
+                    square_s(nx, 1)
+            if grp_now is not None:
+                for i in range(grp_now[0], grp_now[1] + 1):
+                    recs(i)
+                if 0 <= t - 1 < NB:
+                    expo(t - 1)
+            if 0 <= t - 1 < NB:
+                summ(t - 1)
+            if 0 <= t < NB:
+                chain(t)
+                for m in (1, 2, 3):
+                    diff(t, m)
+            if t == 0:
+                quant(1)
+            n1 = t + 1
+            if 0 <= n1 < NB:
+                mx(n1, 1)
+                mx(n1, 2)
+            if f >= 0:
+                gmul(f)
+                final(f, 0)
+                epose(f, 2)
+                final(f, 1)
+                epose(f, 3)
+            if 0 <= n1 < NB:
+                mx(n1, 3)
+            if f >= 0:
+                final(f, 2)
+                final(f, 3)
+                store(f)
+            if t >= 0 and 2 <= t + 2 < NB:
+                quant(t + 2)

@@ -22,10 +22,11 @@ NB = JT // JB
 W = JB * P
 FLOPS = 2 * 2 * B * K * M * D
 
-XL = 3
 GROUPS = ((0, 3), (4, 7), (8, 11), (12, 13), (14, 14), (15, 15))
 LAGX = 4
-SQ_ON_G = True
+LNLAG = 2
+TAIL_TAGS = ("p1", "p2", "p3", "xt0", "xt1", "et0", "et1")
+HEAD_TAGS = ("et0", "et1", "rt", "p1", "p2", "p3")
 
 
 def tile_dota_mix_pa_t_kernel(tc, x, gamma_class, mu, cur_var, pi, out):
@@ -38,7 +39,7 @@ def tile_dota_mix_pa_t_kernel(tc, x, gamma_class, mu, cur_var, pi, out):
     ln_at = {}
     prev = -1
     for a, b in GROUPS:
-        ln_at[b + 2] = (a, b)
+        ln_at[b + LNLAG] = (a, b)
         for i in range(a, b + 1):
             prev = max(prev + 1, b + LAGX)
             fn_at[prev] = i
@@ -57,7 +58,6 @@ def tile_dota_mix_pa_t_kernel(tc, x, gamma_class, mu, cur_var, pi, out):
         psum = ctx.enter_context(tc.psum_pool(name="psum", bufs=1))
 
         identf = const.tile([P, P], F32, name="identf")
-        identb = const.tile([P, P], BF16, name="identb")
         wq = const.tile([P, 2, M, K], U32, name="wq", align_bytes=64)
         ws = const.tile([P, 2, M, K], U8, name="ws", align_bytes=64)
         bd = const.tile([P, M], F32, name="bd")
@@ -77,6 +77,10 @@ def tile_dota_mix_pa_t_kernel(tc, x, gamma_class, mu, cur_var, pi, out):
         et_t = {}
         o_t = {}
         pools = {}
+        state = {"tail": False, "etc": 0}
+
+        def inb(i):
+            return 0 <= i < NB
 
         def load_x(i):
             x_t[i] = xin.tile([P, JB, D], BF16, name="x_sb")
@@ -117,14 +121,26 @@ def tile_dota_mix_pa_t_kernel(tc, x, gamma_class, mu, cur_var, pi, out):
             a = xg_t[i][:, cs, :].rearrange("p c t -> p (c t)")
             eng.tensor_tensor(out=x2g_t[i][:, cs, :].rearrange("p c t -> p (c t)"), in0=a, in1=a, op=ALU.mult)
 
-        def quant(i):
+        def xpath_a(i):
+            words(i, 0, False)
+            square_s(i, 0)
+
+        def xpath_b(i):
+            words(i, 1, False)
+            square_sb(i, slice(2 * P, W), nc.gpsimd)
+
+        def quant_a(i):
             xq = cod.tile([P, W], U32, name="xq", align_bytes=64)
             xs = cod.tile([P, W], U8, name="xs", align_bytes=64)
             x2q = cod.tile([P, W], U32, name="x2q", align_bytes=64)
             x2s = cod.tile([P, W], U8, name="x2s", align_bytes=64)
-            nc.vector.quantize_mx(out=xq[:].bitcast(FP8X4), scales=xs[:], in_=xg_t[i][:].rearrange("p c t -> p (c t)"))
-            nc.vector.quantize_mx(out=x2q[:].bitcast(FP8X4), scales=x2s[:], in_=x2g_t[i][:].rearrange("p c t -> p (c t)"))
             q_t[i] = (x2q, x2s, xq, xs)
+            nc.vector.quantize_mx(out=xq[:].bitcast(FP8X4), scales=xs[:], in_=xg_t[i][:].rearrange("p c t -> p (c t)"))
+
+        def quant_b(i):
+            nc.vector.quantize_mx(
+                out=q_t[i][0][:].bitcast(FP8X4), scales=q_t[i][1][:], in_=x2g_t[i][:].rearrange("p c t -> p (c t)")
+            )
 
         def mx(i, m):
             acc = psum.tile([P, W], F32, tag="p%d" % m, name="acc")
@@ -141,15 +157,15 @@ def tile_dota_mix_pa_t_kernel(tc, x, gamma_class, mu, cur_var, pi, out):
                 )
             pd_t[(i, m)] = acc
 
-        def chain(i):
-            top = tops.tile([P, W], F32, name="top")
-            top_t[i] = top
-            nc.vector.tensor_scalar(
-                out=top[:], in0=pd_t[(i, 1)][:], scalar1=bd[:, 1:2], scalar2=0.0, op0=ALU.add, op1=ALU.max
-            )
-            for m in (2, 3):
+        def chain(i, m):
+            if m == 1:
+                top_t[i] = tops.tile([P, W], F32, name="top")
+                nc.vector.tensor_scalar(
+                    out=top_t[i][:], in0=pd_t[(i, 1)][:], scalar1=bd[:, 1:2], scalar2=0.0, op0=ALU.add, op1=ALU.max
+                )
+            else:
                 nc.vector.scalar_tensor_tensor(
-                    out=top[:], in0=pd_t[(i, m)][:], scalar=bd[:, m : m + 1], in1=top[:], op0=ALU.add, op1=ALU.max
+                    out=top_t[i][:], in0=pd_t[(i, m)][:], scalar=bd[:, m : m + 1], in1=top_t[i][:], op0=ALU.add, op1=ALU.max
                 )
 
         def diff(i, m):
@@ -194,7 +210,12 @@ def tile_dota_mix_pa_t_kernel(tc, x, gamma_class, mu, cur_var, pi, out):
             o_t[i] = outp.tile([P, JB, K * M], F32, name="o_sb")
 
         def epose(i, jl):
-            et = psum.tile([P, M, K], F32, tag="et%d" % (jl % 2), name="et")
+            if state["tail"]:
+                tag = TAIL_TAGS[state["etc"] % len(TAIL_TAGS)]
+                state["etc"] = state["etc"] + 1
+            else:
+                tag = "et%d" % (jl % 2)
+            et = psum.tile([P, M, K], F32, tag=tag, name="et")
             for m in range(M):
                 nc.tensor.transpose(et[:, m, :], de_t[i][:, m, jl * P : (jl + 1) * P], identf[:])
             et_t[(i, jl)] = et
@@ -214,160 +235,219 @@ def tile_dota_mix_pa_t_kernel(tc, x, gamma_class, mu, cur_var, pi, out):
             var_sb = prep.tile([P, M, D], BF16, name="var_sb")
             mu_sb = prep.tile([P, M, D], BF16, name="mu_sb")
             pi_sb = prep.tile([P, M], BF16, name="pi_sb")
-            nc.sync.dma_start(out=var_sb[:], in_=cur_var)
+            nc.scalar.dma_start(out=pi_sb[:], in_=pi)
+            for m in range(M):
+                nc.sync.dma_start(out=var_sb[:, m, :], in_=cur_var[:, m, :])
             load_x(0)
             nc.sync.dma_start(out=mu_sb[:], in_=mu)
-            nc.scalar.dma_start(out=pi_sb[:], in_=pi)
             load_x(1)
             load_x(2)
             load_x(3)
             make_identity(nc, identf[:])
-            make_identity(nc, identb[:])
 
             lnv = prep.tile([P, M, D], F32, name="lnv")
+            y0p = prep.tile([P, M, 4, P], F32, name="y0p")
+            nivp = prep.tile([P, M, 4, P], F32, name="nivp")
+            nmivp = prep.tile([P, M, 4, P], F32, name="nmivp")
+            tmp = prep.tile([P, M, 4, P], F32, name="tmp")
+            wg = prep.tile([P, 2, M, K * 4], BF16, name="wg", align_bytes=64)
             ld = prep.tile([P, M], F32, name="ld")
             pif = prep.tile([P, M], F32, name="pif")
             lnpi = prep.tile([P, M], F32, name="lnpi")
-            niv = prep.tile([P, M, D], F32, name="niv")
-            nmiv = prep.tile([P, M, D], F32, name="nmiv")
-            tmp = prep.tile([P, M, D], F32, name="tmp")
-            w1p = prep.tile([P, M, 4, P], BF16, name="w1p")
-            w2p = prep.tile([P, M, 4, P], BF16, name="w2p")
-            wg = prep.tile([P, 2, M, K * 4], BF16, name="wg", align_bytes=64)
             qs = prep.tile([P, M], F32, name="qs")
             bias = prep.tile([P, M], F32, name="bias")
+            wt_t = {}
 
+            def perm(ap):
+                return ap.rearrange("k (u q e) -> k u e q", u=2, e=2)
+
+            def plan(ap):
+                return ap.rearrange("k (u e) q -> k u e q", e=2)
+
+            def flat(ap):
+                return ap.rearrange("k t q -> k (t q)")
+
+            nc.gpsimd.tensor_scalar(out=pif[:], in0=pi_sb[:], scalar1=1e-10, scalar2=0.0, op0=ALU.add, op1=ALU.add)
             for m in range(M):
                 nc.scalar.activation(out=lnv[:, m, :], in_=var_sb[:, m, :], func=ACT.Ln, accum_out=ld[:, m : m + 1])
-            nc.vector.tensor_scalar_add(out=pif[:], in0=pi_sb[:], scalar1=1e-10)
             nc.scalar.activation(out=lnpi[:], in_=pif[:], func=ACT.Ln)
 
             xpose(0, 0)
             xpose(0, 1)
             words(0, 0, True)
             words(0, 1, True)
-            square_sb(0, slice(0, W), nc.vector)
-            quant(0)
+            square_sb(0, slice(0, W), nc.gpsimd)
+            quant_a(0)
+            xpose(1, 0)
+            xpose(1, 1)
 
             for m in range(M):
-                nc.scalar.activation(out=lnv[:, m, :], in_=lnv[:, m, :], func=ACT.Exp, scale=-1.0)
+                nc.scalar.activation(out=plan(y0p[:, m, :, :]), in_=perm(lnv[:, m, :]), func=ACT.Exp, scale=-1.0)
+            xpath_a(1)
 
             def newton(m):
-                nc.vector.tensor_tensor(out=niv[:, m, :], in0=var_sb[:, m, :], in1=lnv[:, m, :], op=ALU.mult)
+                nc.vector.tensor_tensor(out=plan(nivp[:, m, :, :]), in0=perm(var_sb[:, m, :]), in1=plan(y0p[:, m, :, :]), op=ALU.mult)
                 nc.vector.scalar_tensor_tensor(
-                    out=niv[:, m, :], in0=niv[:, m, :], scalar=2.0, in1=lnv[:, m, :], op0=ALU.subtract, op1=ALU.mult
+                    out=flat(nivp[:, m, :, :]),
+                    in0=flat(nivp[:, m, :, :]),
+                    scalar=2.0,
+                    in1=flat(y0p[:, m, :, :]),
+                    op0=ALU.subtract,
+                    op1=ALU.mult,
                 )
-                nc.vector.tensor_tensor(out=nmiv[:, m, :], in0=mu_sb[:, m, :], in1=niv[:, m, :], op=ALU.mult)
-
-            def casts(m):
-                sign = -1.0 if m == 0 else 1.0
-                nc.scalar.activation(
-                    out=w1p[:, m, :, :].rearrange("k (u e) q -> k u e q", e=2),
-                    in_=niv[:, m, :].rearrange("k (u q e) -> k u e q", u=2, e=2),
-                    func=ACT.Copy,
-                    scale=0.5 * sign,
-                )
-                nc.gpsimd.tensor_scalar(
-                    out=w2p[:, m, :, :].rearrange("k (u e) q -> k u e q", e=2),
-                    in0=nmiv[:, m, :].rearrange("k (u q e) -> k u e q", u=2, e=2),
-                    scalar1=-1.0 * sign,
-                    scalar2=0.0,
-                    op0=ALU.mult,
-                    op1=ALU.add,
-                )
-                nc.gpsimd.tensor_tensor(out=tmp[:, m, :], in0=nmiv[:, m, :], in1=mu_sb[:, m, :], op=ALU.mult)
+                nc.vector.tensor_tensor(out=plan(nmivp[:, m, :, :]), in0=perm(mu_sb[:, m, :]), in1=plan(nivp[:, m, :, :]), op=ALU.mult)
+                nc.gpsimd.tensor_tensor(out=plan(tmp[:, m, :, :]), in0=perm(mu_sb[:, m, :]), in1=plan(nmivp[:, m, :, :]), op=ALU.mult)
 
             def wpose(m):
-                for w, wp in enumerate((w1p, w2p)):
-                    wt = psum.tile([P, 4, K], BF16, tag="et%d" % w, name="wt")
+                for w, src in enumerate((nivp, nmivp)):
+                    wt = psum.tile([P, 4, K], F32, tag=HEAD_TAGS[(2 * m + w) % len(HEAD_TAGS)], name="wt")
                     for t in range(4):
-                        nc.tensor.transpose(wt[:, t, :], wp[:, m, t, :], identb[:])
-                    nc.scalar.copy(out=wg[:, w, m, :].rearrange("p (k t) -> p k t", t=4), in_=wt[:].rearrange("p t k -> p k t"))
+                        nc.tensor.transpose(wt[:, t, :], src[:, m, t, :], identf[:])
+                    wt_t[(m, w)] = wt
+
+            def wcast(m):
+                sign = -1.0 if m == 0 else 1.0
+                for w, sc in enumerate((0.5 * sign, -1.0 * sign)):
+                    nc.scalar.activation(
+                        out=wg[:, w, m, :].rearrange("p (k t) -> p k t", t=4),
+                        in_=wt_t[(m, w)][:].rearrange("p t k -> p k t"),
+                        func=ACT.Copy,
+                        scale=sc,
+                    )
 
             def wquant(m):
                 for w in range(2):
                     nc.vector.quantize_mx(out=wq[:, w, m, :].bitcast(FP8X4), scales=ws[:, w, m, :], in_=wg[:, w, m, :])
 
+            def wsum(m):
+                nc.scalar.activation(out=flat(tmp[:, m, :, :]), in_=flat(tmp[:, m, :, :]), func=ACT.Copy, accum_out=qs[:, m : m + 1])
+
             newton(0)
-            casts(0)
-            newton(1)
-            casts(1)
             wpose(0)
-            newton(2)
-            casts(2)
+            wcast(0)
+            wsum(0)
+            newton(1)
             wpose(1)
+            wcast(1)
+            wsum(1)
+            newton(2)
+            wpose(2)
+            wcast(2)
+            wsum(2)
+            quant_b(0)
             wquant(0)
             newton(3)
-            casts(3)
-            wpose(2)
-            wquant(1)
             wpose(3)
+            wsum(3)
+            wcast(3)
+            wquant(1)
+            mx(0, 1)
             wquant(2)
-            wquant(3)
-            for m in range(M):
-                nc.scalar.activation(out=tmp[:, m, :], in_=tmp[:, m, :], func=ACT.Copy, accum_out=qs[:, m : m + 1])
+            mx(0, 2)
             nc.vector.tensor_tensor(out=qs[:], in0=qs[:], in1=ld[:], op=ALU.subtract)
             nc.vector.scalar_tensor_tensor(out=bias[:], in0=qs[:], scalar=0.5, in1=lnpi[:], op0=ALU.mult, op1=ALU.add)
             nc.vector.tensor_scalar(out=bd[:], in0=bias[:], scalar1=bias[:, 0:1], scalar2=None, op0=ALU.subtract)
+            wquant(3)
+            mx(0, 3)
+            xpath_b(1)
+            xpose(2, 0)
+            xpose(2, 1)
+            xpath_a(2)
+            xpath_b(2)
 
         pools["big"] = ctx.enter_context(tc.tile_pool(name="big", bufs=8))
 
-        for t in range(-2, last_step + 1):
+        for t in range(0, last_step + 1):
             f = fn_at.get(t, -1)
-            nx = t + XL
-            if XL + 1 <= nx + 1 < NB:
-                load_x(nx + 1)
-            if 0 <= t < 4:
+            f2 = fn_at.get(t + 1, -1)
+            a = t + 3
+            if t >= NB - 1:
+                state["tail"] = True
+            if inb(a + 1):
+                load_x(a + 1)
+            if t < 4:
                 load_g(t)
-            if f >= 0:
-                rpose(f)
-                epose(f, 0)
-                epose(f, 1)
-            if 1 <= nx < NB:
-                xpose(nx, 0)
-                xpose(nx, 1)
+            if inb(t - 1):
+                expo(t - 1)
+                summ(t - 1)
+            if state["tail"]:
+                if inb(t):
+                    for m in (1, 2, 3):
+                        chain(t, m)
+                    for m in (1, 2, 3):
+                        diff(t, m)
+                if f >= 0:
+                    epose(f, 2)
+                    epose(f, 3)
+                if f2 >= 0:
+                    rpose(f2)
+                    epose(f2, 0)
+                    epose(f2, 1)
+                if f >= 0:
+                    for jl in range(JB):
+                        final(f, jl)
+                    store(f)
+                if f2 >= 0:
+                    gmul(f2)
+            elif f < 0:
+                for m in (1, 2, 3):
+                    chain(t, m)
+                if inb(a):
+                    xpose(a, 0)
+                    xpose(a, 1)
+                if f2 >= 0:
+                    rpose(f2)
+                for m in (1, 2, 3):
+                    diff(t, m)
+                if t == 0:
+                    quant_a(1)
+                    quant_b(1)
+                mx(t + 1, 1)
+                if f2 >= 0:
+                    epose(f2, 0)
+                mx(t + 1, 2)
+                if f2 >= 0:
+                    epose(f2, 1)
+                mx(t + 1, 3)
+                quant_a(t + 2)
+                quant_b(t + 2)
+                if f2 >= 0:
+                    gmul(f2)
+            else:
+                chain(t, 1)
+                final(f, 0)
+                chain(t, 2)
+                final(f, 1)
+                chain(t, 3)
+                epose(f, 2)
+                if inb(a):
+                    xpose(a, 0)
+                epose(f, 3)
+                if inb(a):
+                    xpose(a, 1)
+                rpose(f2)
+                if inb(t + 2):
+                    quant_a(t + 2)
+                diff(t, 1)
+                final(f, 2)
+                diff(t, 2)
+                final(f, 3)
+                store(f)
+                diff(t, 3)
+                if inb(t + 2):
+                    quant_b(t + 2)
+                mx(t + 1, 1)
+                epose(f2, 0)
+                mx(t + 1, 2)
+                epose(f2, 1)
+                mx(t + 1, 3)
+                gmul(f2)
+            if inb(a):
+                xpath_a(a)
+                xpath_b(a)
             grp_now = ln_at.get(t, None)
             if grp_now is not None:
                 for i in range(grp_now[0], grp_now[1] + 1):
                     logs(i)
-            elif 0 <= t - 1 < NB:
-                expo(t - 1)
-            if 1 <= nx < NB:
-                words(nx, 0, False)
-                square_s(nx, 0)
-                words(nx, 1, False)
-                if SQ_ON_G:
-                    square_sb(nx, slice(2 * P, W), nc.gpsimd)
-                else:
-                    square_s(nx, 1)
-            if grp_now is not None:
                 for i in range(grp_now[0], grp_now[1] + 1):
                     recs(i)
-                if 0 <= t - 1 < NB:
-                    expo(t - 1)
-            if 0 <= t - 1 < NB:
-                summ(t - 1)
-            if 0 <= t < NB:
-                chain(t)
-                for m in (1, 2, 3):
-                    diff(t, m)
-            if t == 0:
-                quant(1)
-            n1 = t + 1
-            if 0 <= n1 < NB:
-                mx(n1, 1)
-                mx(n1, 2)
-            if f >= 0:
-                gmul(f)
-                final(f, 0)
-                epose(f, 2)
-                final(f, 1)
-                epose(f, 3)
-            if 0 <= n1 < NB:
-                mx(n1, 3)
-            if f >= 0:
-                final(f, 2)
-                final(f, 3)
-                store(f)
-            if t >= 0 and 2 <= t + 2 < NB:
-                quant(t + 2)

@@ -25,8 +25,9 @@ FLOPS = 2 * 2 * B * K * M * D
 GROUPS = ((0, 3), (4, 7), (8, 11), (12, 13), (14, 14), (15, 15))
 LAGX = 4
 LNLAG = 2
-TAIL_TAGS = ("p1", "p2", "p3", "xt0", "xt1", "et0", "et1")
-HEAD_TAGS = ("et0", "et1", "rt", "p1", "p2", "p3")
+TAIL_TAGS = ("acc", "acc", "acc", "acc", "xt0", "et0", "et1")
+HEAD_TAGS = ("acc", "acc", "acc", "acc", "et0", "et1")
+XT_TAGS = ("xt0", "xr")
 
 
 def tile_dota_mix_pa_t_kernel(tc, x, gamma_class, mu, cur_var, pi, out):
@@ -56,6 +57,7 @@ def tile_dota_mix_pa_t_kernel(tc, x, gamma_class, mu, cur_var, pi, out):
         sums = ctx.enter_context(tc.tile_pool(name="sums", bufs=8))
         outp = ctx.enter_context(tc.tile_pool(name="outp", bufs=3))
         psum = ctx.enter_context(tc.psum_pool(name="psum", bufs=1))
+        pacc = ctx.enter_context(tc.psum_pool(name="pacc", bufs=4))
 
         identf = const.tile([P, P], F32, name="identf")
         wq = const.tile([P, 2, M, K], U32, name="wq", align_bytes=64)
@@ -82,6 +84,11 @@ def tile_dota_mix_pa_t_kernel(tc, x, gamma_class, mu, cur_var, pi, out):
         def inb(i):
             return 0 <= i < NB
 
+        def bank(tag, shape, name):
+            if tag == "acc":
+                return pacc.tile(shape, F32, tag="acc", name=name)
+            return psum.tile(shape, F32, tag=tag, name=name)
+
         def load_x(i):
             x_t[i] = xin.tile([P, JB, D], BF16, name="x_sb")
             nc.sync.dma_start(out=x_t[i][:], in_=xv[:, i * JB : (i + 1) * JB, :])
@@ -90,7 +97,7 @@ def tile_dota_mix_pa_t_kernel(tc, x, gamma_class, mu, cur_var, pi, out):
             nc.sync.dma_start(out=g_sb[:, c * 16 : (c + 1) * 16, :], in_=gv[:, c * 16 : (c + 1) * 16, :])
 
         def xpose(i, h):
-            xt = psum.tile([P, 2, 2 * P], F32, tag="xt%d" % h, name="xt")
+            xt = psum.tile([P, 2, 2 * P], F32, tag=XT_TAGS[h], name="xt")
             xw = x_t[i][:].bitcast(F32)
             for jj in range(2):
                 for u in range(2):
@@ -143,7 +150,7 @@ def tile_dota_mix_pa_t_kernel(tc, x, gamma_class, mu, cur_var, pi, out):
             )
 
         def mx(i, m):
-            acc = psum.tile([P, W], F32, tag="p%d" % m, name="acc")
+            acc = pacc.tile([P, W], F32, tag="acc", name="acc")
             passes = ((0, m), (0, 0), (1, m), (1, 0))
             for n, (w, mm) in enumerate(passes):
                 nc.tensor.matmul_mx(
@@ -199,7 +206,7 @@ def tile_dota_mix_pa_t_kernel(tc, x, gamma_class, mu, cur_var, pi, out):
             nc.scalar.activation(out=s_t[i][:], in_=s_t[i][:], func=ACT.Exp, scale=-1.0)
 
         def rpose(i):
-            rt = psum.tile([P, JB, K], F32, tag="rt", name="rt")
+            rt = psum.tile([P, JB, K], F32, tag="xr", name="rt")
             for jl in range(JB):
                 nc.tensor.transpose(rt[:, jl, :], s_t[i][:, jl * P : (jl + 1) * P], identf[:])
             rt_t[i] = rt
@@ -215,7 +222,7 @@ def tile_dota_mix_pa_t_kernel(tc, x, gamma_class, mu, cur_var, pi, out):
                 state["etc"] = state["etc"] + 1
             else:
                 tag = "et%d" % (jl % 2)
-            et = psum.tile([P, M, K], F32, tag=tag, name="et")
+            et = bank(tag, [P, M, K], "et")
             for m in range(M):
                 nc.tensor.transpose(et[:, m, :], de_t[i][:, m, jl * P : (jl + 1) * P], identf[:])
             et_t[(i, jl)] = et
@@ -300,7 +307,7 @@ def tile_dota_mix_pa_t_kernel(tc, x, gamma_class, mu, cur_var, pi, out):
 
             def wpose(m):
                 for w, src in enumerate((nivp, nmivp)):
-                    wt = psum.tile([P, 4, K], F32, tag=HEAD_TAGS[(2 * m + w) % len(HEAD_TAGS)], name="wt")
+                    wt = bank(HEAD_TAGS[(2 * m + w) % len(HEAD_TAGS)], [P, 4, K], "wt")
                     for t in range(4):
                         nc.tensor.transpose(wt[:, t, :], src[:, m, t, :], identf[:])
                     wt_t[(m, w)] = wt
@@ -390,58 +397,61 @@ def tile_dota_mix_pa_t_kernel(tc, x, gamma_class, mu, cur_var, pi, out):
                 if f2 >= 0:
                     gmul(f2)
             elif f < 0:
-                for m in (1, 2, 3):
-                    chain(t, m)
-                if inb(a):
-                    xpose(a, 0)
-                    xpose(a, 1)
-                if f2 >= 0:
-                    rpose(f2)
-                for m in (1, 2, 3):
-                    diff(t, m)
+                chain(t, 1)
+                if t > 0:
+                    mx(t + 1, 1)
+                chain(t, 2)
+                chain(t, 3)
                 if t == 0:
                     quant_a(1)
                     quant_b(1)
-                mx(t + 1, 1)
+                    mx(t + 1, 1)
+                xpose(a, 0)
+                diff(t, 1)
                 if f2 >= 0:
-                    epose(f2, 0)
+                    rpose(f2)
                 mx(t + 1, 2)
                 if f2 >= 0:
-                    epose(f2, 1)
+                    gmul(f2)
+                diff(t, 2)
+                if f2 >= 0:
+                    epose(f2, 0)
+                xpose(a, 1)
                 mx(t + 1, 3)
+                if f2 >= 0:
+                    epose(f2, 1)
+                diff(t, 3)
                 quant_a(t + 2)
                 quant_b(t + 2)
-                if f2 >= 0:
-                    gmul(f2)
             else:
                 chain(t, 1)
                 final(f, 0)
+                epose(f, 2)
+                mx(t + 1, 1)
                 chain(t, 2)
                 final(f, 1)
                 chain(t, 3)
-                epose(f, 2)
-                if inb(a):
-                    xpose(a, 0)
-                epose(f, 3)
-                if inb(a):
-                    xpose(a, 1)
-                rpose(f2)
                 if inb(t + 2):
                     quant_a(t + 2)
                 diff(t, 1)
                 final(f, 2)
+                epose(f, 3)
+                if inb(a):
+                    xpose(a, 0)
+                rpose(f2)
+                mx(t + 1, 2)
+                gmul(f2)
                 diff(t, 2)
                 final(f, 3)
                 store(f)
                 diff(t, 3)
                 if inb(t + 2):
                     quant_b(t + 2)
-                mx(t + 1, 1)
                 epose(f2, 0)
-                mx(t + 1, 2)
-                epose(f2, 1)
+                if inb(a):
+                    xpose(a, 1)
                 mx(t + 1, 3)
-                gmul(f2)
+                epose(f2, 1)
             if inb(a):
                 xpath_a(a)
                 xpath_b(a)

@@ -25,9 +25,8 @@ FLOPS = 2 * 2 * B * K * M * D
 GROUPS = ((0, 3), (4, 7), (8, 11), (12, 13), (14, 14), (15, 15))
 LAGX = 4
 LNLAG = 2
-TAIL_TAGS = ("acc", "acc", "acc", "acc", "xt0", "et0", "et1")
-HEAD_TAGS = ("acc", "acc", "acc", "acc", "et0", "et1")
-XT_TAGS = ("xt0", "xr")
+TAIL_TAGS = ("p1", "p2", "p3", "xt0", "xt1", "et0", "et1")
+HEAD_TAGS = ("et0", "et1", "rt", "p1", "p2", "p3")
 
 
 def tile_dota_mix_pa_t_kernel(tc, x, gamma_class, mu, cur_var, pi, out):
@@ -57,7 +56,6 @@ def tile_dota_mix_pa_t_kernel(tc, x, gamma_class, mu, cur_var, pi, out):
         sums = ctx.enter_context(tc.tile_pool(name="sums", bufs=8))
         outp = ctx.enter_context(tc.tile_pool(name="outp", bufs=3))
         psum = ctx.enter_context(tc.psum_pool(name="psum", bufs=1))
-        pacc = ctx.enter_context(tc.psum_pool(name="pacc", bufs=4))
 
         identf = const.tile([P, P], F32, name="identf")
         wq = const.tile([P, 2, M, K], U32, name="wq", align_bytes=64)
@@ -84,11 +82,6 @@ def tile_dota_mix_pa_t_kernel(tc, x, gamma_class, mu, cur_var, pi, out):
         def inb(i):
             return 0 <= i < NB
 
-        def bank(tag, shape, name):
-            if tag == "acc":
-                return pacc.tile(shape, F32, tag="acc", name=name)
-            return psum.tile(shape, F32, tag=tag, name=name)
-
         def load_x(i):
             x_t[i] = xin.tile([P, JB, D], BF16, name="x_sb")
             nc.sync.dma_start(out=x_t[i][:], in_=xv[:, i * JB : (i + 1) * JB, :])
@@ -97,7 +90,7 @@ def tile_dota_mix_pa_t_kernel(tc, x, gamma_class, mu, cur_var, pi, out):
             nc.sync.dma_start(out=g_sb[:, c * 16 : (c + 1) * 16, :], in_=gv[:, c * 16 : (c + 1) * 16, :])
 
         def xpose(i, h):
-            xt = psum.tile([P, 2, 2 * P], F32, tag=XT_TAGS[h], name="xt")
+            xt = psum.tile([P, 2, 2 * P], F32, tag="xt%d" % h, name="xt")
             xw = x_t[i][:].bitcast(F32)
             for jj in range(2):
                 for u in range(2):
@@ -134,7 +127,7 @@ def tile_dota_mix_pa_t_kernel(tc, x, gamma_class, mu, cur_var, pi, out):
 
         def xpath_b(i):
             words(i, 1, False)
-            square_sb(i, slice(2 * P, W), nc.gpsimd)
+            square_s(i, 1)
 
         def quant_a(i):
             xq = cod.tile([P, W], U32, name="xq", align_bytes=64)
@@ -150,7 +143,7 @@ def tile_dota_mix_pa_t_kernel(tc, x, gamma_class, mu, cur_var, pi, out):
             )
 
         def mx(i, m):
-            acc = pacc.tile([P, W], F32, tag="acc", name="acc")
+            acc = psum.tile([P, W], F32, tag="p%d" % m, name="acc")
             passes = ((0, m), (0, 0), (1, m), (1, 0))
             for n, (w, mm) in enumerate(passes):
                 nc.tensor.matmul_mx(
@@ -206,7 +199,7 @@ def tile_dota_mix_pa_t_kernel(tc, x, gamma_class, mu, cur_var, pi, out):
             nc.scalar.activation(out=s_t[i][:], in_=s_t[i][:], func=ACT.Exp, scale=-1.0)
 
         def rpose(i):
-            rt = psum.tile([P, JB, K], F32, tag="xr", name="rt")
+            rt = psum.tile([P, JB, K], F32, tag="rt", name="rt")
             for jl in range(JB):
                 nc.tensor.transpose(rt[:, jl, :], s_t[i][:, jl * P : (jl + 1) * P], identf[:])
             rt_t[i] = rt
@@ -222,7 +215,7 @@ def tile_dota_mix_pa_t_kernel(tc, x, gamma_class, mu, cur_var, pi, out):
                 state["etc"] = state["etc"] + 1
             else:
                 tag = "et%d" % (jl % 2)
-            et = bank(tag, [P, M, K], "et")
+            et = psum.tile([P, M, K], F32, tag=tag, name="et")
             for m in range(M):
                 nc.tensor.transpose(et[:, m, :], de_t[i][:, m, jl * P : (jl + 1) * P], identf[:])
             et_t[(i, jl)] = et
@@ -307,7 +300,7 @@ def tile_dota_mix_pa_t_kernel(tc, x, gamma_class, mu, cur_var, pi, out):
 
             def wpose(m):
                 for w, src in enumerate((nivp, nmivp)):
-                    wt = bank(HEAD_TAGS[(2 * m + w) % len(HEAD_TAGS)], [P, 4, K], "wt")
+                    wt = psum.tile([P, 4, K], F32, tag=HEAD_TAGS[(2 * m + w) % len(HEAD_TAGS)], name="wt")
                     for t in range(4):
                         nc.tensor.transpose(wt[:, t, :], src[:, m, t, :], identf[:])
                     wt_t[(m, w)] = wt
@@ -397,61 +390,58 @@ def tile_dota_mix_pa_t_kernel(tc, x, gamma_class, mu, cur_var, pi, out):
                 if f2 >= 0:
                     gmul(f2)
             elif f < 0:
-                chain(t, 1)
-                if t > 0:
-                    mx(t + 1, 1)
-                chain(t, 2)
-                chain(t, 3)
+                for m in (1, 2, 3):
+                    chain(t, m)
+                if inb(a):
+                    xpose(a, 0)
+                    xpose(a, 1)
+                if f2 >= 0:
+                    rpose(f2)
+                for m in (1, 2, 3):
+                    diff(t, m)
                 if t == 0:
                     quant_a(1)
                     quant_b(1)
-                    mx(t + 1, 1)
-                xpose(a, 0)
-                diff(t, 1)
-                if f2 >= 0:
-                    rpose(f2)
-                mx(t + 1, 2)
-                if f2 >= 0:
-                    gmul(f2)
-                diff(t, 2)
+                mx(t + 1, 1)
                 if f2 >= 0:
                     epose(f2, 0)
-                xpose(a, 1)
-                mx(t + 1, 3)
+                mx(t + 1, 2)
                 if f2 >= 0:
                     epose(f2, 1)
-                diff(t, 3)
+                mx(t + 1, 3)
                 quant_a(t + 2)
                 quant_b(t + 2)
+                if f2 >= 0:
+                    gmul(f2)
             else:
                 chain(t, 1)
                 final(f, 0)
-                epose(f, 2)
-                mx(t + 1, 1)
                 chain(t, 2)
                 final(f, 1)
                 chain(t, 3)
+                epose(f, 2)
+                if inb(a):
+                    xpose(a, 0)
+                epose(f, 3)
+                if inb(a):
+                    xpose(a, 1)
+                rpose(f2)
                 if inb(t + 2):
                     quant_a(t + 2)
                 diff(t, 1)
                 final(f, 2)
-                epose(f, 3)
-                if inb(a):
-                    xpose(a, 0)
-                rpose(f2)
-                mx(t + 1, 2)
-                gmul(f2)
                 diff(t, 2)
                 final(f, 3)
                 store(f)
                 diff(t, 3)
                 if inb(t + 2):
                     quant_b(t + 2)
+                mx(t + 1, 1)
                 epose(f2, 0)
-                if inb(a):
-                    xpose(a, 1)
-                mx(t + 1, 3)
+                mx(t + 1, 2)
                 epose(f2, 1)
+                mx(t + 1, 3)
+                gmul(f2)
             if inb(a):
                 xpath_a(a)
                 xpath_b(a)

@@ -22,7 +22,7 @@ NB = JT // JB
 W = JB * P
 FLOPS = 2 * 2 * B * K * M * D
 
-GROUPS = ((0, 3), (4, 7), (8, 11), (12, 13), (14, 14), (15, 15))
+GROUPS = ((0, 3), (4, 7), (8, 11), (12, 15))
 LAGX = 4
 LNLAG = 2
 TAIL_TAGS = ("p1", "p2", "p3", "xt0", "xt1", "et0", "et1")
@@ -361,7 +361,7 @@ def tile_dota_mix_pa_t_kernel(tc, x, gamma_class, mu, cur_var, pi, out):
             f = fn_at.get(t, -1)
             f2 = fn_at.get(t + 1, -1)
             a = t + 3
-            if t >= NB - 1:
+            if t >= NB:
                 state["tail"] = True
             if inb(a + 1):
                 load_x(a + 1)
@@ -370,77 +370,54 @@ def tile_dota_mix_pa_t_kernel(tc, x, gamma_class, mu, cur_var, pi, out):
             if inb(t - 1):
                 expo(t - 1)
                 summ(t - 1)
-            if state["tail"]:
-                if inb(t):
-                    for m in (1, 2, 3):
-                        chain(t, m)
-                    for m in (1, 2, 3):
-                        diff(t, m)
-                if f >= 0:
-                    epose(f, 2)
-                    epose(f, 3)
-                if f2 >= 0:
-                    rpose(f2)
-                    epose(f2, 0)
-                    epose(f2, 1)
-                if f >= 0:
-                    for jl in range(JB):
-                        final(f, jl)
-                    store(f)
-                if f2 >= 0:
-                    gmul(f2)
-            elif f < 0:
-                for m in (1, 2, 3):
-                    chain(t, m)
-                if inb(a):
-                    xpose(a, 0)
-                    xpose(a, 1)
-                if f2 >= 0:
-                    rpose(f2)
-                for m in (1, 2, 3):
-                    diff(t, m)
-                if t == 0:
-                    quant_a(1)
-                    quant_b(1)
-                mx(t + 1, 1)
-                if f2 >= 0:
-                    epose(f2, 0)
-                mx(t + 1, 2)
-                if f2 >= 0:
-                    epose(f2, 1)
-                mx(t + 1, 3)
-                quant_a(t + 2)
-                quant_b(t + 2)
-                if f2 >= 0:
-                    gmul(f2)
-            else:
+            if inb(t):
                 chain(t, 1)
+            if f >= 0:
                 final(f, 0)
+            if inb(t):
                 chain(t, 2)
+            if f >= 0:
                 final(f, 1)
+            if inb(t):
                 chain(t, 3)
+            if f >= 0:
                 epose(f, 2)
-                if inb(a):
-                    xpose(a, 0)
+            if inb(a):
+                xpose(a, 0)
+            if f >= 0:
                 epose(f, 3)
-                if inb(a):
-                    xpose(a, 1)
+            if inb(a):
+                xpose(a, 1)
+            if f2 >= 0:
                 rpose(f2)
-                if inb(t + 2):
-                    quant_a(t + 2)
+            if inb(t):
                 diff(t, 1)
+            if f >= 0:
                 final(f, 2)
+            if inb(t):
                 diff(t, 2)
+            if f >= 0:
                 final(f, 3)
                 store(f)
+            if inb(t):
                 diff(t, 3)
-                if inb(t + 2):
-                    quant_b(t + 2)
+            if t == 0:
+                quant_a(1)
+                quant_b(1)
+            if inb(t + 1):
                 mx(t + 1, 1)
+            if f2 >= 0:
                 epose(f2, 0)
+            if inb(t + 1):
                 mx(t + 1, 2)
+            if f2 >= 0:
                 epose(f2, 1)
+            if inb(t + 1):
                 mx(t + 1, 3)
+            if inb(t + 2):
+                quant_a(t + 2)
+                quant_b(t + 2)
+            if f2 >= 0:
                 gmul(f2)
             if inb(a):
                 xpath_a(a)

@@ -117,10 +117,6 @@ def tile_dota_mix_pa_t_kernel(tc, x, gamma_class, mu, cur_var, pi, out):
                 func=ACT.Square,
             )
 
-        def square_sb(i, cs, eng):
-            a = xg_t[i][:, cs, :].rearrange("p c t -> p (c t)")
-            eng.tensor_tensor(out=x2g_t[i][:, cs, :].rearrange("p c t -> p (c t)"), in0=a, in1=a, op=ALU.mult)
-
         def xpath_a(i):
             words(i, 0, False)
             square_s(i, 0)
@@ -228,8 +224,8 @@ def tile_dota_mix_pa_t_kernel(tc, x, gamma_class, mu, cur_var, pi, out):
                 op=ALU.mult,
             )
 
-        def store(i):
-            nc.sync.dma_start(out=ov[:, i * JB : (i + 1) * JB, :], in_=o_t[i][:])
+        def store(i, jl):
+            nc.sync.dma_start(out=ov[:, i * JB + jl, :], in_=o_t[i][:, jl, :])
 
         with tc.tile_pool(name="prep", bufs=1) as prep:
             var_sb = prep.tile([P, M, D], BF16, name="var_sb")
@@ -276,14 +272,14 @@ def tile_dota_mix_pa_t_kernel(tc, x, gamma_class, mu, cur_var, pi, out):
             xpose(0, 1)
             words(0, 0, True)
             words(0, 1, True)
-            square_sb(0, slice(0, W), nc.gpsimd)
             quant_a(0)
-            xpose(1, 0)
-            xpose(1, 1)
 
             for m in range(M):
                 nc.scalar.activation(out=plan(y0p[:, m, :, :]), in_=perm(lnv[:, m, :]), func=ACT.Exp, scale=-1.0)
-            xpath_a(1)
+            square_s(0, 0)
+            square_s(0, 1)
+            xpose(1, 0)
+            xpose(1, 1)
 
             def newton(m):
                 nc.vector.tensor_tensor(out=plan(nivp[:, m, :, :]), in0=perm(var_sb[:, m, :]), in1=plan(y0p[:, m, :, :]), op=ALU.mult)
@@ -349,6 +345,7 @@ def tile_dota_mix_pa_t_kernel(tc, x, gamma_class, mu, cur_var, pi, out):
             nc.vector.tensor_scalar(out=bd[:], in0=bias[:], scalar1=bias[:, 0:1], scalar2=None, op0=ALU.subtract)
             wquant(3)
             mx(0, 3)
+            xpath_a(1)
             xpath_b(1)
             xpose(2, 0)
             xpose(2, 1)
@@ -374,10 +371,12 @@ def tile_dota_mix_pa_t_kernel(tc, x, gamma_class, mu, cur_var, pi, out):
                 chain(t, 1)
             if f >= 0:
                 final(f, 0)
+                store(f, 0)
             if inb(t):
                 chain(t, 2)
             if f >= 0:
                 final(f, 1)
+                store(f, 1)
             if inb(t):
                 chain(t, 3)
             if f >= 0:
@@ -394,11 +393,12 @@ def tile_dota_mix_pa_t_kernel(tc, x, gamma_class, mu, cur_var, pi, out):
                 diff(t, 1)
             if f >= 0:
                 final(f, 2)
+                store(f, 2)
             if inb(t):
                 diff(t, 2)
             if f >= 0:
                 final(f, 3)
-                store(f)
+                store(f, 3)
             if inb(t):
                 diff(t, 3)
             if t == 0:

@@ -12,38 +12,34 @@ ALU = mybir.AluOpType
 ACT = mybir.ActivationFunctionType
 
 P = 128
-B = 8192
-K = 128
-M = 4
-D = 512
-JT = B // P
-JB = 4
-NB = JT // JB
-W = JB * P
-FLOPS = 2 * 2 * B * K * M * D
+SAMPLES = 8192
+CLASSES = 128
+MODES = 4
+FEATURES = 512
+PACK = 4
+TILES = SAMPLES // P
+TILES_PER_BLOCK = 4
+BLOCKS = TILES // TILES_PER_BLOCK
+BLOCK = TILES_PER_BLOCK * P
+HALF = BLOCK // 2
+GAMMA_LOADS = 4
+FLOPS = 2 * 2 * SAMPLES * CLASSES * MODES * FEATURES
 
-GROUPS = ((0, 3), (4, 7), (8, 11), (12, 15))
-LAGX = 4
-LNLAG = 2
-TAIL_TAGS = ("p1", "p2", "p3", "xt0", "xt1", "et0", "et1")
-HEAD_TAGS = ("et0", "et1", "rt", "p1", "p2", "p3")
+AHEAD = 3
+GROUP = 4
+LN_DELAY = 2
+LAG = (GROUP - 1) + LN_DELAY + 2
+
+WEIGHT_BANKS = ("et0", "et1", "rt", "p1", "p2", "p3")
+DRAIN_BANKS = ("p1", "p2", "p3", "xt0", "xt1", "et0", "et1")
+FIRST_DRAIN_TILE = TILES_PER_BLOCK * (BLOCKS - LAG) + 2
 
 
 def tile_dota_mix_pa_t_kernel(tc, x, gamma_class, mu, cur_var, pi, out):
     nc = tc.nc
-    xv = x.rearrange("(p j) d -> p j d", j=JT)
-    gv = gamma_class.rearrange("(p j) k -> p j k", j=JT)
-    ov = out.rearrange("(p j) k m -> p j (k m)", j=JT)
-
-    fn_at = {}
-    ln_at = {}
-    prev = -1
-    for a, b in GROUPS:
-        ln_at[b + LNLAG] = (a, b)
-        for i in range(a, b + 1):
-            prev = max(prev + 1, b + LAGX)
-            fn_at[prev] = i
-    last_step = prev
+    x_rows = x.rearrange("(p j) d -> p j d", j=TILES)
+    gamma_rows = gamma_class.rearrange("(p j) k -> p j k", j=TILES)
+    out_rows = out.rearrange("(p j) k m -> p j (k m)", j=TILES)
 
     with ExitStack() as ctx:
         ctx.enter_context(tc.manual_schedule())
@@ -53,378 +49,346 @@ def tile_dota_mix_pa_t_kernel(tc, x, gamma_class, mu, cur_var, pi, out):
         cod = ctx.enter_context(tc.tile_pool(name="cod", bufs=3))
         two = ctx.enter_context(tc.tile_pool(name="two", bufs=2))
         tops = ctx.enter_context(tc.tile_pool(name="tops", bufs=4))
-        sums = ctx.enter_context(tc.tile_pool(name="sums", bufs=8))
+        sums = ctx.enter_context(tc.tile_pool(name="sums", bufs=LAG + 1))
         outp = ctx.enter_context(tc.tile_pool(name="outp", bufs=3))
         psum = ctx.enter_context(tc.psum_pool(name="psum", bufs=1))
 
-        identf = const.tile([P, P], F32, name="identf")
-        wq = const.tile([P, 2, M, K], U32, name="wq", align_bytes=64)
-        ws = const.tile([P, 2, M, K], U8, name="ws", align_bytes=64)
-        bd = const.tile([P, M], F32, name="bd")
-        g_sb = const.tile([P, JT, K], BF16, name="g_sb")
+        identity = const.tile([P, P], F32, name="identf")
+        w_words = const.tile([P, 2, MODES, CLASSES], U32, name="wq", align_bytes=64)
+        w_scales = const.tile([P, 2, MODES, CLASSES], U8, name="ws", align_bytes=64)
+        dbias = const.tile([P, MODES], F32, name="bd")
+        gamma_sb = const.tile([P, TILES, CLASSES], BF16, name="g_sb")
 
+        x_sb = {}
         x_t = {}
-        xt_t = {}
-        xg_t = {}
-        x2g_t = {}
-        q_t = {}
-        pd_t = {}
-        top_t = {}
-        de_t = {}
-        s_t = {}
-        rt_t = {}
-        rr_t = {}
-        et_t = {}
-        o_t = {}
-        pools = {}
-        state = {"tail": False, "etc": 0}
+        x_grouped = {}
+        xx_grouped = {}
+        operands = {}
+        group_acc = {}
+        top = {}
+        expo = {}
+        esum = {}
+        rsum_t = {}
+        ratio = {}
+        expo_t = {}
+        result = {}
 
-        def inb(i):
-            return 0 <= i < NB
+        def is_block(i):
+            return 0 <= i < BLOCKS
+
 
         def load_x(i):
-            x_t[i] = xin.tile([P, JB, D], BF16, name="x_sb")
-            nc.sync.dma_start(out=x_t[i][:], in_=xv[:, i * JB : (i + 1) * JB, :])
+            x_sb[i] = xin.tile([P, TILES_PER_BLOCK, FEATURES], BF16, name="x_sb")
+            nc.sync.dma_start(out=x_sb[i][:], in_=x_rows[:, i * TILES_PER_BLOCK : (i + 1) * TILES_PER_BLOCK, :])
 
-        def load_g(c):
-            nc.sync.dma_start(out=g_sb[:, c * 16 : (c + 1) * 16, :], in_=gv[:, c * 16 : (c + 1) * 16, :])
+        def load_gamma(c):
+            js = slice(c * TILES // GAMMA_LOADS, (c + 1) * TILES // GAMMA_LOADS)
+            nc.sync.dma_start(out=gamma_sb[:, js, :], in_=gamma_rows[:, js, :])
 
-        def xpose(i, h):
-            xt = psum.tile([P, 2, 2 * P], F32, tag="xt%d" % h, name="xt")
-            xw = x_t[i][:].bitcast(F32)
+        def transpose_x(i, h):
+            x_t[(i, h)] = psum.tile([P, 2, HALF], F32, tag="xt%d" % h, name="xt")
+            pairs = x_sb[i][:].bitcast(F32)
             for jj in range(2):
                 for u in range(2):
-                    nc.tensor.transpose(xt[:, u, jj * P : (jj + 1) * P], xw[:, 2 * h + jj, u * P : (u + 1) * P], identf[:])
-            xt_t[(i, h)] = xt
+                    nc.tensor.transpose(
+                        x_t[(i, h)][:, u, jj * P : (jj + 1) * P], pairs[:, 2 * h + jj, u * P : (u + 1) * P], identity[:]
+                    )
 
-        def words(i, h, on_vector):
+        def copy_x(i, h, on_vector):
             if h == 0:
-                xg_t[i] = grp.tile([P, W, 4], BF16, name="xg", align_bytes=64)
-                x2g_t[i] = grp.tile([P, W, 4], BF16, name="x2g", align_bytes=64)
-            cs = slice(h * 2 * P, (h + 1) * 2 * P)
-            dst = xg_t[i][:].bitcast(F32)[:, cs, :]
-            src = xt_t[(i, h)][:].rearrange("p u c -> p c u")
+                x_grouped[i] = grp.tile([P, BLOCK, PACK], BF16, name="xg", align_bytes=64)
+                xx_grouped[i] = grp.tile([P, BLOCK, PACK], BF16, name="x2g", align_bytes=64)
+            cols = slice(h * HALF, (h + 1) * HALF)
+            dst = x_grouped[i][:].bitcast(F32)[:, cols, :]
+            src = x_t[(i, h)][:].rearrange("p u c -> p c u")
             if on_vector:
                 nc.vector.tensor_copy(out=dst, in_=src)
             else:
                 nc.scalar.copy(out=dst, in_=src)
 
-        def square_s(i, h):
-            cs = slice(h * 2 * P, (h + 1) * 2 * P)
+        def square_x(i, h):
+            cols = slice(h * HALF, (h + 1) * HALF)
             nc.scalar.activation(
-                out=x2g_t[i][:, cs, :].rearrange("p c (u e) -> p c u e", e=2),
-                in_=xt_t[(i, h)][:].bitcast(BF16).rearrange("p u (c e) -> p c u e", e=2),
+                out=xx_grouped[i][:, cols, :].rearrange("p c (u e) -> p c u e", e=2),
+                in_=x_t[(i, h)][:].bitcast(BF16).rearrange("p u (c e) -> p c u e", e=2),
                 func=ACT.Square,
             )
 
-        def xpath_a(i):
-            words(i, 0, False)
-            square_s(i, 0)
+        def copy_and_square_x(i):
+            for h in range(2):
+                copy_x(i, h, False)
+                square_x(i, h)
 
-        def xpath_b(i):
-            words(i, 1, False)
-            square_s(i, 1)
-
-        def quant_a(i):
-            xq = cod.tile([P, W], U32, name="xq", align_bytes=64)
-            xs = cod.tile([P, W], U8, name="xs", align_bytes=64)
-            x2q = cod.tile([P, W], U32, name="x2q", align_bytes=64)
-            x2s = cod.tile([P, W], U8, name="x2s", align_bytes=64)
-            q_t[i] = (x2q, x2s, xq, xs)
-            nc.vector.quantize_mx(out=xq[:].bitcast(FP8X4), scales=xs[:], in_=xg_t[i][:].rearrange("p c t -> p (c t)"))
-
-        def quant_b(i):
+        def quantise_x(i):
+            x_words = cod.tile([P, BLOCK], U32, name="xq", align_bytes=64)
+            x_scales = cod.tile([P, BLOCK], U8, name="xs", align_bytes=64)
+            xx_words = cod.tile([P, BLOCK], U32, name="x2q", align_bytes=64)
+            xx_scales = cod.tile([P, BLOCK], U8, name="x2s", align_bytes=64)
+            operands[i] = ((xx_words, xx_scales), (x_words, x_scales))
             nc.vector.quantize_mx(
-                out=q_t[i][0][:].bitcast(FP8X4), scales=q_t[i][1][:], in_=x2g_t[i][:].rearrange("p c t -> p (c t)")
+                out=x_words[:].bitcast(FP8X4), scales=x_scales[:], in_=x_grouped[i][:].rearrange("p c t -> p (c t)")
             )
 
-        def mx(i, m):
-            acc = psum.tile([P, W], F32, tag="p%d" % m, name="acc")
-            passes = ((0, m), (0, 0), (1, m), (1, 0))
-            for n, (w, mm) in enumerate(passes):
-                nc.tensor.matmul_mx(
-                    out=acc[:],
-                    lhsT=wq[:, w, mm, :].bitcast(FP8X4),
-                    lhsT_scale=ws[:, w, mm, :],
-                    rhs=q_t[i][2 * w][:].bitcast(FP8X4),
-                    rhs_scale=q_t[i][2 * w + 1][:],
-                    start=(n == 0),
-                    stop=(n == 3),
-                )
-            pd_t[(i, m)] = acc
+        def quantise_xx(i):
+            xx_words, xx_scales = operands[i][0]
+            nc.vector.quantize_mx(
+                out=xx_words[:].bitcast(FP8X4), scales=xx_scales[:], in_=xx_grouped[i][:].rearrange("p c t -> p (c t)")
+            )
 
-        def chain(i, m):
+
+        def mx_group(i, m):
+            group_acc[(i, m)] = psum.tile([P, BLOCK], F32, tag="p%d" % m, name="acc")
+            passes = ((0, m), (0, 0), (1, m), (1, 0))
+            for n, (w, mode) in enumerate(passes):
+                words, scales = operands[i][w]
+                nc.tensor.matmul_mx(
+                    out=group_acc[(i, m)][:],
+                    lhsT=w_words[:, w, mode, :].bitcast(FP8X4),
+                    lhsT_scale=w_scales[:, w, mode, :],
+                    rhs=words[:].bitcast(FP8X4),
+                    rhs_scale=scales[:],
+                    start=(n == 0),
+                    stop=(n == len(passes) - 1),
+                )
+
+        def running_max(i, m):
             if m == 1:
-                top_t[i] = tops.tile([P, W], F32, name="top")
+                top[i] = tops.tile([P, BLOCK], F32, name="top")
                 nc.vector.tensor_scalar(
-                    out=top_t[i][:], in0=pd_t[(i, 1)][:], scalar1=bd[:, 1:2], scalar2=0.0, op0=ALU.add, op1=ALU.max
+                    out=top[i][:], in0=group_acc[(i, 1)][:], scalar1=dbias[:, 1:2], scalar2=0.0, op0=ALU.add, op1=ALU.max
                 )
             else:
                 nc.vector.scalar_tensor_tensor(
-                    out=top_t[i][:], in0=pd_t[(i, m)][:], scalar=bd[:, m : m + 1], in1=top_t[i][:], op0=ALU.add, op1=ALU.max
+                    out=top[i][:],
+                    in0=group_acc[(i, m)][:],
+                    scalar=dbias[:, m : m + 1],
+                    in1=top[i][:],
+                    op0=ALU.add,
+                    op1=ALU.max,
                 )
 
-        def diff(i, m):
+        def subtract_max(i, m):
             if m == 1:
-                de_t[i] = pools["big"].tile([P, M, W], F32, name="de")
+                expo[i] = big.tile([P, MODES, BLOCK], F32, name="de")
             nc.vector.scalar_tensor_tensor(
-                out=de_t[i][:, m, :],
-                in0=pd_t[(i, m)][:],
-                scalar=bd[:, m : m + 1],
-                in1=top_t[i][:],
+                out=expo[i][:, m, :],
+                in0=group_acc[(i, m)][:],
+                scalar=dbias[:, m : m + 1],
+                in1=top[i][:],
                 op0=ALU.add,
                 op1=ALU.subtract,
             )
 
-        def expo(i):
-            de = de_t[i]
-            nc.scalar.activation(out=de[:, 0, :], in_=top_t[i][:], func=ACT.Exp, scale=-1.0)
-            nc.scalar.activation(out=de[:, 1:4, :], in_=de[:, 1:4, :], func=ACT.Exp)
+        def exponentials(i):
+            nc.scalar.activation(out=expo[i][:, 0, :], in_=top[i][:], func=ACT.Exp, scale=-1.0)
+            nc.scalar.activation(out=expo[i][:, 1:4, :], in_=expo[i][:, 1:4, :], func=ACT.Exp)
 
-        def summ(i):
-            de = de_t[i]
-            hs = two.tile([P, 2, W], F32, name="hs")
-            nc.gpsimd.tensor_tensor(out=hs[:], in0=de[:, 0:2, :], in1=de[:, 2:4, :], op=ALU.add)
-            s_t[i] = sums.tile([P, W], F32, name="ssum")
-            nc.gpsimd.tensor_tensor(out=s_t[i][:], in0=hs[:, 0, :], in1=hs[:, 1, :], op=ALU.add)
+        def sum_modes(i):
+            half_sums = two.tile([P, 2, BLOCK], F32, name="hs")
+            nc.gpsimd.tensor_tensor(out=half_sums[:], in0=expo[i][:, 0:2, :], in1=expo[i][:, 2:4, :], op=ALU.add)
+            esum[i] = sums.tile([P, BLOCK], F32, name="ssum")
+            nc.gpsimd.tensor_tensor(out=esum[i][:], in0=half_sums[:, 0, :], in1=half_sums[:, 1, :], op=ALU.add)
 
-        def logs(i):
-            nc.scalar.activation(out=s_t[i][:], in_=s_t[i][:], func=ACT.Ln)
+        def reciprocal_sums(first):
+            for i in range(first, first + GROUP):
+                nc.scalar.activation(out=esum[i][:], in_=esum[i][:], func=ACT.Ln)
+            for i in range(first, first + GROUP):
+                nc.scalar.activation(out=esum[i][:], in_=esum[i][:], func=ACT.Exp, scale=-1.0)
 
-        def recs(i):
-            nc.scalar.activation(out=s_t[i][:], in_=s_t[i][:], func=ACT.Exp, scale=-1.0)
 
-        def rpose(i):
-            rt = psum.tile([P, JB, K], F32, tag="rt", name="rt")
-            for jl in range(JB):
-                nc.tensor.transpose(rt[:, jl, :], s_t[i][:, jl * P : (jl + 1) * P], identf[:])
-            rt_t[i] = rt
+        def transpose_rsum(i):
+            rsum_t[i] = psum.tile([P, TILES_PER_BLOCK, CLASSES], F32, tag="rt", name="rt")
+            for jl in range(TILES_PER_BLOCK):
+                nc.tensor.transpose(rsum_t[i][:, jl, :], esum[i][:, jl * P : (jl + 1) * P], identity[:])
 
-        def gmul(i):
-            rr_t[i] = two.tile([P, JB, K], F32, name="rr")
-            nc.vector.tensor_tensor(out=rr_t[i][:], in0=rt_t[i][:], in1=g_sb[:, i * JB : (i + 1) * JB, :], op=ALU.mult)
-            o_t[i] = outp.tile([P, JB, K * M], F32, name="o_sb")
+        def times_gamma(i):
+            ratio[i] = two.tile([P, TILES_PER_BLOCK, CLASSES], F32, name="rr")
+            js = slice(i * TILES_PER_BLOCK, (i + 1) * TILES_PER_BLOCK)
+            nc.vector.tensor_tensor(out=ratio[i][:], in0=rsum_t[i][:], in1=gamma_sb[:, js, :], op=ALU.mult)
+            result[i] = outp.tile([P, TILES_PER_BLOCK, CLASSES * MODES], F32, name="o_sb")
 
-        def epose(i, jl):
-            if state["tail"]:
-                tag = TAIL_TAGS[state["etc"] % len(TAIL_TAGS)]
-                state["etc"] = state["etc"] + 1
-            else:
-                tag = "et%d" % (jl % 2)
-            et = psum.tile([P, M, K], F32, tag=tag, name="et")
-            for m in range(M):
-                nc.tensor.transpose(et[:, m, :], de_t[i][:, m, jl * P : (jl + 1) * P], identf[:])
-            et_t[(i, jl)] = et
+        def transpose_expo(i, jl):
+            drained = TILES_PER_BLOCK * i + jl - FIRST_DRAIN_TILE
+            bank = DRAIN_BANKS[drained % len(DRAIN_BANKS)] if drained >= 0 else "et%d" % (jl % 2)
+            expo_t[(i, jl)] = psum.tile([P, MODES, CLASSES], F32, tag=bank, name="et")
+            for m in range(MODES):
+                nc.tensor.transpose(expo_t[(i, jl)][:, m, :], expo[i][:, m, jl * P : (jl + 1) * P], identity[:])
 
-        def final(i, jl):
+        def finish_tile(i, jl):
             nc.vector.tensor_tensor(
-                out=o_t[i][:, jl, :].rearrange("p (k m) -> p k m", m=M),
-                in0=et_t[(i, jl)][:].rearrange("p m k -> p k m"),
-                in1=rr_t[i][:, jl, :].unsqueeze(2).to_broadcast([P, K, M]),
+                out=result[i][:, jl, :].rearrange("p (k m) -> p k m", m=MODES),
+                in0=expo_t[(i, jl)][:].rearrange("p m k -> p k m"),
+                in1=ratio[i][:, jl, :].unsqueeze(2).to_broadcast([P, CLASSES, MODES]),
                 op=ALU.mult,
             )
-
-        def store(i, jl):
-            nc.sync.dma_start(out=ov[:, i * JB + jl, :], in_=o_t[i][:, jl, :])
+            nc.sync.dma_start(out=out_rows[:, i * TILES_PER_BLOCK + jl, :], in_=result[i][:, jl, :])
 
         with tc.tile_pool(name="prep", bufs=1) as prep:
-            var_sb = prep.tile([P, M, D], BF16, name="var_sb")
-            mu_sb = prep.tile([P, M, D], BF16, name="mu_sb")
-            pi_sb = prep.tile([P, M], BF16, name="pi_sb")
+            var_sb = prep.tile([P, MODES, FEATURES], BF16, name="var_sb")
+            mu_sb = prep.tile([P, MODES, FEATURES], BF16, name="mu_sb")
+            pi_sb = prep.tile([P, MODES], BF16, name="pi_sb")
             nc.scalar.dma_start(out=pi_sb[:], in_=pi)
-            for m in range(M):
+            for m in range(MODES):
                 nc.sync.dma_start(out=var_sb[:, m, :], in_=cur_var[:, m, :])
             load_x(0)
             nc.sync.dma_start(out=mu_sb[:], in_=mu)
-            load_x(1)
-            load_x(2)
-            load_x(3)
-            make_identity(nc, identf[:])
+            for i in range(1, AHEAD + 1):
+                load_x(i)
+            make_identity(nc, identity[:])
 
-            lnv = prep.tile([P, M, D], F32, name="lnv")
-            y0p = prep.tile([P, M, 4, P], F32, name="y0p")
-            nivp = prep.tile([P, M, 4, P], F32, name="nivp")
-            nmivp = prep.tile([P, M, 4, P], F32, name="nmivp")
-            tmp = prep.tile([P, M, 4, P], F32, name="tmp")
-            wg = prep.tile([P, 2, M, K * 4], BF16, name="wg", align_bytes=64)
-            ld = prep.tile([P, M], F32, name="ld")
-            pif = prep.tile([P, M], F32, name="pif")
-            lnpi = prep.tile([P, M], F32, name="lnpi")
-            qs = prep.tile([P, M], F32, name="qs")
-            bias = prep.tile([P, M], F32, name="bias")
-            wt_t = {}
+            ln_var = prep.tile([P, MODES, FEATURES], F32, name="lnv")
+            seed = prep.tile([P, MODES, PACK, P], F32, name="y0p")
+            neg_iv = prep.tile([P, MODES, PACK, P], F32, name="nivp")
+            neg_mu_iv = prep.tile([P, MODES, PACK, P], F32, name="nmivp")
+            neg_mu2_iv = prep.tile([P, MODES, PACK, P], F32, name="tmp")
+            w_grouped = prep.tile([P, 2, MODES, CLASSES * PACK], BF16, name="wg", align_bytes=64)
+            log_det = prep.tile([P, MODES], F32, name="ld")
+            pi_eps = prep.tile([P, MODES], F32, name="pif")
+            ln_pi = prep.tile([P, MODES], F32, name="lnpi")
+            neg_quad = prep.tile([P, MODES], F32, name="qs")
+            bias = prep.tile([P, MODES], F32, name="bias")
+            w_t = {}
 
-            def perm(ap):
+            def by_value(ap):
                 return ap.rearrange("k (u q e) -> k u e q", u=2, e=2)
 
-            def plan(ap):
+            def split(ap):
                 return ap.rearrange("k (u e) q -> k u e q", e=2)
 
             def flat(ap):
                 return ap.rearrange("k t q -> k (t q)")
 
-            nc.gpsimd.tensor_scalar(out=pif[:], in0=pi_sb[:], scalar1=1e-10, scalar2=0.0, op0=ALU.add, op1=ALU.add)
-            for m in range(M):
-                nc.scalar.activation(out=lnv[:, m, :], in_=var_sb[:, m, :], func=ACT.Ln, accum_out=ld[:, m : m + 1])
-            nc.scalar.activation(out=lnpi[:], in_=pif[:], func=ACT.Ln)
+            nc.gpsimd.tensor_scalar(out=pi_eps[:], in0=pi_sb[:], scalar1=1e-10, scalar2=0.0, op0=ALU.add, op1=ALU.add)
+            for m in range(MODES):
+                nc.scalar.activation(
+                    out=ln_var[:, m, :], in_=var_sb[:, m, :], func=ACT.Ln, accum_out=log_det[:, m : m + 1]
+                )
+            nc.scalar.activation(out=ln_pi[:], in_=pi_eps[:], func=ACT.Ln)
 
-            xpose(0, 0)
-            xpose(0, 1)
-            words(0, 0, True)
-            words(0, 1, True)
-            quant_a(0)
+            for h in range(2):
+                transpose_x(0, h)
+            for h in range(2):
+                copy_x(0, h, True)
+            quantise_x(0)
 
-            for m in range(M):
-                nc.scalar.activation(out=plan(y0p[:, m, :, :]), in_=perm(lnv[:, m, :]), func=ACT.Exp, scale=-1.0)
-            square_s(0, 0)
-            square_s(0, 1)
-            xpose(1, 0)
-            xpose(1, 1)
+            for m in range(MODES):
+                nc.scalar.activation(out=split(seed[:, m, :, :]), in_=by_value(ln_var[:, m, :]), func=ACT.Exp, scale=-1.0)
+            for h in range(2):
+                square_x(0, h)
+            for h in range(2):
+                transpose_x(1, h)
 
-            def newton(m):
-                nc.vector.tensor_tensor(out=plan(nivp[:, m, :, :]), in0=perm(var_sb[:, m, :]), in1=plan(y0p[:, m, :, :]), op=ALU.mult)
+            for m in range(MODES):
+                nc.vector.tensor_tensor(
+                    out=split(neg_iv[:, m, :, :]), in0=by_value(var_sb[:, m, :]), in1=split(seed[:, m, :, :]), op=ALU.mult
+                )
                 nc.vector.scalar_tensor_tensor(
-                    out=flat(nivp[:, m, :, :]),
-                    in0=flat(nivp[:, m, :, :]),
+                    out=flat(neg_iv[:, m, :, :]),
+                    in0=flat(neg_iv[:, m, :, :]),
                     scalar=2.0,
-                    in1=flat(y0p[:, m, :, :]),
+                    in1=flat(seed[:, m, :, :]),
                     op0=ALU.subtract,
                     op1=ALU.mult,
                 )
-                nc.vector.tensor_tensor(out=plan(nmivp[:, m, :, :]), in0=perm(mu_sb[:, m, :]), in1=plan(nivp[:, m, :, :]), op=ALU.mult)
-                nc.gpsimd.tensor_tensor(out=plan(tmp[:, m, :, :]), in0=perm(mu_sb[:, m, :]), in1=plan(nmivp[:, m, :, :]), op=ALU.mult)
-
-            def wpose(m):
-                for w, src in enumerate((nivp, nmivp)):
-                    wt = psum.tile([P, 4, K], F32, tag=HEAD_TAGS[(2 * m + w) % len(HEAD_TAGS)], name="wt")
-                    for t in range(4):
-                        nc.tensor.transpose(wt[:, t, :], src[:, m, t, :], identf[:])
-                    wt_t[(m, w)] = wt
-
-            def wcast(m):
+                nc.vector.tensor_tensor(
+                    out=split(neg_mu_iv[:, m, :, :]), in0=by_value(mu_sb[:, m, :]), in1=split(neg_iv[:, m, :, :]), op=ALU.mult
+                )
+                nc.gpsimd.tensor_tensor(
+                    out=split(neg_mu2_iv[:, m, :, :]),
+                    in0=by_value(mu_sb[:, m, :]),
+                    in1=split(neg_mu_iv[:, m, :, :]),
+                    op=ALU.mult,
+                )
                 sign = -1.0 if m == 0 else 1.0
-                for w, sc in enumerate((0.5 * sign, -1.0 * sign)):
-                    nc.scalar.activation(
-                        out=wg[:, w, m, :].rearrange("p (k t) -> p k t", t=4),
-                        in_=wt_t[(m, w)][:].rearrange("p t k -> p k t"),
-                        func=ACT.Copy,
-                        scale=sc,
+                for w, src in enumerate((neg_iv, neg_mu_iv)):
+                    w_t[w] = psum.tile(
+                        [P, PACK, CLASSES], F32, tag=WEIGHT_BANKS[(2 * m + w) % len(WEIGHT_BANKS)], name="wt"
                     )
+                    for t in range(PACK):
+                        nc.tensor.transpose(w_t[w][:, t, :], src[:, m, t, :], identity[:])
+                for w, factor in enumerate((0.5 * sign, -1.0 * sign)):
+                    nc.scalar.activation(
+                        out=w_grouped[:, w, m, :].rearrange("p (k t) -> p k t", t=PACK),
+                        in_=w_t[w][:].rearrange("p t k -> p k t"),
+                        func=ACT.Copy,
+                        scale=factor,
+                    )
+                nc.scalar.activation(
+                    out=flat(neg_mu2_iv[:, m, :, :]),
+                    in_=flat(neg_mu2_iv[:, m, :, :]),
+                    func=ACT.Copy,
+                    accum_out=neg_quad[:, m : m + 1],
+                )
 
-            def wquant(m):
+            quantise_xx(0)
+            for m in range(MODES):
                 for w in range(2):
-                    nc.vector.quantize_mx(out=wq[:, w, m, :].bitcast(FP8X4), scales=ws[:, w, m, :], in_=wg[:, w, m, :])
+                    nc.vector.quantize_mx(
+                        out=w_words[:, w, m, :].bitcast(FP8X4), scales=w_scales[:, w, m, :], in_=w_grouped[:, w, m, :]
+                    )
+                if m >= 1:
+                    mx_group(0, m)
 
-            def wsum(m):
-                nc.scalar.activation(out=flat(tmp[:, m, :, :]), in_=flat(tmp[:, m, :, :]), func=ACT.Copy, accum_out=qs[:, m : m + 1])
+            nc.vector.tensor_tensor(out=neg_quad[:], in0=neg_quad[:], in1=log_det[:], op=ALU.subtract)
+            nc.vector.scalar_tensor_tensor(
+                out=bias[:], in0=neg_quad[:], scalar=0.5, in1=ln_pi[:], op0=ALU.mult, op1=ALU.add
+            )
+            nc.vector.tensor_scalar(out=dbias[:], in0=bias[:], scalar1=bias[:, 0:1], scalar2=None, op0=ALU.subtract)
 
-            newton(0)
-            wpose(0)
-            wcast(0)
-            wsum(0)
-            newton(1)
-            wpose(1)
-            wcast(1)
-            wsum(1)
-            newton(2)
-            wpose(2)
-            wcast(2)
-            wsum(2)
-            quant_b(0)
-            wquant(0)
-            newton(3)
-            wpose(3)
-            wsum(3)
-            wcast(3)
-            wquant(1)
-            mx(0, 1)
-            wquant(2)
-            mx(0, 2)
-            nc.vector.tensor_tensor(out=qs[:], in0=qs[:], in1=ld[:], op=ALU.subtract)
-            nc.vector.scalar_tensor_tensor(out=bias[:], in0=qs[:], scalar=0.5, in1=lnpi[:], op0=ALU.mult, op1=ALU.add)
-            nc.vector.tensor_scalar(out=bd[:], in0=bias[:], scalar1=bias[:, 0:1], scalar2=None, op0=ALU.subtract)
-            wquant(3)
-            mx(0, 3)
-            xpath_a(1)
-            xpath_b(1)
-            xpose(2, 0)
-            xpose(2, 1)
-            xpath_a(2)
-            xpath_b(2)
+            copy_and_square_x(1)
+            for h in range(2):
+                transpose_x(2, h)
+            copy_and_square_x(2)
 
-        pools["big"] = ctx.enter_context(tc.tile_pool(name="big", bufs=8))
+        big = ctx.enter_context(tc.tile_pool(name="big", bufs=LAG + 1))
 
-        for t in range(0, last_step + 1):
-            f = fn_at.get(t, -1)
-            f2 = fn_at.get(t + 1, -1)
-            a = t + 3
-            if t >= NB:
-                state["tail"] = True
-            if inb(a + 1):
-                load_x(a + 1)
-            if t < 4:
-                load_g(t)
-            if inb(t - 1):
-                expo(t - 1)
-                summ(t - 1)
-            if inb(t):
-                chain(t, 1)
-            if f >= 0:
-                final(f, 0)
-                store(f, 0)
-            if inb(t):
-                chain(t, 2)
-            if f >= 0:
-                final(f, 1)
-                store(f, 1)
-            if inb(t):
-                chain(t, 3)
-            if f >= 0:
-                epose(f, 2)
-            if inb(a):
-                xpose(a, 0)
-            if f >= 0:
-                epose(f, 3)
-            if inb(a):
-                xpose(a, 1)
-            if f2 >= 0:
-                rpose(f2)
-            if inb(t):
-                diff(t, 1)
-            if f >= 0:
-                final(f, 2)
-                store(f, 2)
-            if inb(t):
-                diff(t, 2)
-            if f >= 0:
-                final(f, 3)
-                store(f, 3)
-            if inb(t):
-                diff(t, 3)
+        for t in range(BLOCKS + LAG):
+            done = t - LAG
+            if is_block(t + AHEAD + 1):
+                load_x(t + AHEAD + 1)
+            if t < GAMMA_LOADS:
+                load_gamma(t)
+            if is_block(t - 1):
+                exponentials(t - 1)
+                sum_modes(t - 1)
+            for n in range(2):
+                if is_block(t):
+                    running_max(t, n + 1)
+                if is_block(done):
+                    finish_tile(done, n)
+            if is_block(t):
+                running_max(t, 3)
+            for n in range(2):
+                if is_block(done):
+                    transpose_expo(done, n + 2)
+                if is_block(t + AHEAD):
+                    transpose_x(t + AHEAD, n)
+            if is_block(done + 1):
+                transpose_rsum(done + 1)
+            for n in range(2):
+                if is_block(t):
+                    subtract_max(t, n + 1)
+                if is_block(done):
+                    finish_tile(done, n + 2)
+            if is_block(t):
+                subtract_max(t, 3)
             if t == 0:
-                quant_a(1)
-                quant_b(1)
-            if inb(t + 1):
-                mx(t + 1, 1)
-            if f2 >= 0:
-                epose(f2, 0)
-            if inb(t + 1):
-                mx(t + 1, 2)
-            if f2 >= 0:
-                epose(f2, 1)
-            if inb(t + 1):
-                mx(t + 1, 3)
-            if inb(t + 2):
-                quant_a(t + 2)
-                quant_b(t + 2)
-            if f2 >= 0:
-                gmul(f2)
-            if inb(a):
-                xpath_a(a)
-                xpath_b(a)
-            grp_now = ln_at.get(t, None)
-            if grp_now is not None:
-                for i in range(grp_now[0], grp_now[1] + 1):
-                    logs(i)
-                for i in range(grp_now[0], grp_now[1] + 1):
-                    recs(i)
+                quantise_x(1)
+                quantise_xx(1)
+            for n in range(2):
+                if is_block(t + 1):
+                    mx_group(t + 1, n + 1)
+                if is_block(done + 1):
+                    transpose_expo(done + 1, n)
+            if is_block(t + 1):
+                mx_group(t + 1, 3)
+            if is_block(t + 2):
+                quantise_x(t + 2)
+                quantise_xx(t + 2)
+            if is_block(done + 1):
+                times_gamma(done + 1)
+            if is_block(t + AHEAD):
+                copy_and_square_x(t + AHEAD)
+            first = t - LN_DELAY - (GROUP - 1)
+            if is_block(first) and first % GROUP == 0:
+                reciprocal_sums(first)

from contextlib import ExitStack

import concourse.mybir as mybir
from concourse.masks import make_identity

F32 = mybir.dt.float32
BF16 = mybir.dt.bfloat16
U32 = mybir.dt.uint32
U8 = mybir.dt.uint8
FP8X4 = mybir.dt.float8_e4m3fn_x4
ALU = mybir.AluOpType
ACT = mybir.ActivationFunctionType

P = 128
SAMPLES = 8192
CLASSES = 128
MODES = 4
FEATURES = 512
PACK = 4
TILES = SAMPLES // P
TILES_PER_BLOCK = 4
BLOCKS = TILES // TILES_PER_BLOCK
BLOCK = TILES_PER_BLOCK * P
HALF = BLOCK // 2
GAMMA_LOADS = 4
FLOPS = 2 * 2 * SAMPLES * CLASSES * MODES * FEATURES

AHEAD = 3
GROUP = 4
LN_DELAY = 2
LAG = (GROUP - 1) + LN_DELAY + 2

WEIGHT_BANKS = ("et0", "et1", "rt", "p1", "p2", "p3")
DRAIN_BANKS = ("p1", "p2", "p3", "xt0", "xt1", "et0", "et1")
FIRST_DRAIN_TILE = TILES_PER_BLOCK * (BLOCKS - LAG) + 2


def tile_dota_mix_pa_t_kernel(tc, x, gamma_class, mu, cur_var, pi, out):
    nc = tc.nc
    x_rows = x.rearrange("(p j) d -> p j d", j=TILES)
    gamma_rows = gamma_class.rearrange("(p j) k -> p j k", j=TILES)
    out_rows = out.rearrange("(p j) k m -> p j (k m)", j=TILES)

    with ExitStack() as ctx:
        ctx.enter_context(tc.manual_schedule())
        const = ctx.enter_context(tc.tile_pool(name="const", bufs=1))
        xin = ctx.enter_context(tc.tile_pool(name="xin", bufs=4))
        grp = ctx.enter_context(tc.tile_pool(name="grp", bufs=3))
        cod = ctx.enter_context(tc.tile_pool(name="cod", bufs=3))
        two = ctx.enter_context(tc.tile_pool(name="two", bufs=2))
        tops = ctx.enter_context(tc.tile_pool(name="tops", bufs=4))
        sums = ctx.enter_context(tc.tile_pool(name="sums", bufs=LAG + 1))
        outp = ctx.enter_context(tc.tile_pool(name="outp", bufs=3))
        psum = ctx.enter_context(tc.psum_pool(name="psum", bufs=1))

        identity = const.tile([P, P], F32, name="identf")
        w_words = const.tile([P, 2, MODES, CLASSES], U32, name="wq", align_bytes=64)
        w_scales = const.tile([P, 2, MODES, CLASSES], U8, name="ws", align_bytes=64)
        dbias = const.tile([P, MODES], F32, name="bd")
        gamma_sb = const.tile([P, TILES, CLASSES], BF16, name="g_sb")

        x_sb = {}
        x_t = {}
        x_grouped = {}
        xx_grouped = {}
        operands = {}
        group_acc = {}
        top = {}
        expo = {}
        esum = {}
        rsum_t = {}
        ratio = {}
        expo_t = {}
        result = {}

        def is_block(i):
            return 0 <= i < BLOCKS


        def load_x(i):
            x_sb[i] = xin.tile([P, TILES_PER_BLOCK, FEATURES], BF16, name="x_sb")
            nc.sync.dma_start(out=x_sb[i][:], in_=x_rows[:, i * TILES_PER_BLOCK : (i + 1) * TILES_PER_BLOCK, :])

        def load_gamma(c):
            js = slice(c * TILES // GAMMA_LOADS, (c + 1) * TILES // GAMMA_LOADS)
            nc.sync.dma_start(out=gamma_sb[:, js, :], in_=gamma_rows[:, js, :])

        def transpose_x(i, h):
            x_t[(i, h)] = psum.tile([P, 2, HALF], F32, tag="xt%d" % h, name="xt")
            pairs = x_sb[i][:].bitcast(F32)
            for jj in range(2):
                for u in range(2):
                    nc.tensor.transpose(
                        x_t[(i, h)][:, u, jj * P : (jj + 1) * P], pairs[:, 2 * h + jj, u * P : (u + 1) * P], identity[:]
                    )

        def copy_x(i, h, on_vector):
            if h == 0:
                x_grouped[i] = grp.tile([P, BLOCK, PACK], BF16, name="xg", align_bytes=64)
                xx_grouped[i] = grp.tile([P, BLOCK, PACK], BF16, name="x2g", align_bytes=64)
            cols = slice(h * HALF, (h + 1) * HALF)
            dst = x_grouped[i][:].bitcast(F32)[:, cols, :]
            src = x_t[(i, h)][:].rearrange("p u c -> p c u")
            if on_vector:
                nc.vector.tensor_copy(out=dst, in_=src)
            else:
                nc.scalar.copy(out=dst, in_=src)

        def square_x(i, h):
            cols = slice(h * HALF, (h + 1) * HALF)
            nc.scalar.activation(
                out=xx_grouped[i][:, cols, :].rearrange("p c (u e) -> p c u e", e=2),
                in_=x_t[(i, h)][:].bitcast(BF16).rearrange("p u (c e) -> p c u e", e=2),
                func=ACT.Square,
            )

        def copy_and_square_x(i):
            for h in range(2):
                copy_x(i, h, False)
                square_x(i, h)

        def quantise_x(i):
            x_words = cod.tile([P, BLOCK], U32, name="xq", align_bytes=64)
            x_scales = cod.tile([P, BLOCK], U8, name="xs", align_bytes=64)
            xx_words = cod.tile([P, BLOCK], U32, name="x2q", align_bytes=64)
            xx_scales = cod.tile([P, BLOCK], U8, name="x2s", align_bytes=64)
            operands[i] = ((xx_words, xx_scales), (x_words, x_scales))
            nc.vector.quantize_mx(
                out=x_words[:].bitcast(FP8X4), scales=x_scales[:], in_=x_grouped[i][:].rearrange("p c t -> p (c t)")
            )

        def quantise_xx(i):
            xx_words, xx_scales = operands[i][0]
            nc.vector.quantize_mx(
                out=xx_words[:].bitcast(FP8X4), scales=xx_scales[:], in_=xx_grouped[i][:].rearrange("p c t -> p (c t)")
            )


        def mx_group(i, m):
            group_acc[(i, m)] = psum.tile([P, BLOCK], F32, tag="p%d" % m, name="acc")
            passes = ((0, m), (0, 0), (1, m), (1, 0))
            for n, (w, mode) in enumerate(passes):
                words, scales = operands[i][w]
                nc.tensor.matmul_mx(
                    out=group_acc[(i, m)][:],
                    lhsT=w_words[:, w, mode, :].bitcast(FP8X4),
                    lhsT_scale=w_scales[:, w, mode, :],
                    rhs=words[:].bitcast(FP8X4),
                    rhs_scale=scales[:],
                    start=(n == 0),
                    stop=(n == len(passes) - 1),
                )

        def running_max(i, m):
            if m == 1:
                top[i] = tops.tile([P, BLOCK], F32, name="top")
                nc.vector.tensor_scalar(
                    out=top[i][:], in0=group_acc[(i, 1)][:], scalar1=dbias[:, 1:2], scalar2=0.0, op0=ALU.add, op1=ALU.max
                )
            else:
                nc.vector.scalar_tensor_tensor(
                    out=top[i][:],
                    in0=group_acc[(i, m)][:],
                    scalar=dbias[:, m : m + 1],
                    in1=top[i][:],
                    op0=ALU.add,
                    op1=ALU.max,
                )

        def subtract_max(i, m):
            if m == 1:
                expo[i] = big.tile([P, MODES, BLOCK], F32, name="de")
            nc.vector.scalar_tensor_tensor(
                out=expo[i][:, m, :],
                in0=group_acc[(i, m)][:],
                scalar=dbias[:, m : m + 1],
                in1=top[i][:],
                op0=ALU.add,
                op1=ALU.subtract,
            )

        def exponentials(i):
            nc.scalar.activation(out=expo[i][:, 0, :], in_=top[i][:], func=ACT.Exp, scale=-1.0)
            nc.scalar.activation(out=expo[i][:, 1:4, :], in_=expo[i][:, 1:4, :], func=ACT.Exp)

        def sum_modes(i):
            half_sums = two.tile([P, 2, BLOCK], F32, name="hs")
            nc.gpsimd.tensor_tensor(out=half_sums[:], in0=expo[i][:, 0:2, :], in1=expo[i][:, 2:4, :], op=ALU.add)
            esum[i] = sums.tile([P, BLOCK], F32, name="ssum")
            nc.gpsimd.tensor_tensor(out=esum[i][:], in0=half_sums[:, 0, :], in1=half_sums[:, 1, :], op=ALU.add)

        def reciprocal_sums(first):
            for i in range(first, first + GROUP):
                nc.scalar.activation(out=esum[i][:], in_=esum[i][:], func=ACT.Ln)
            for i in range(first, first + GROUP):
                nc.scalar.activation(out=esum[i][:], in_=esum[i][:], func=ACT.Exp, scale=-1.0)


        def transpose_rsum(i):
            rsum_t[i] = psum.tile([P, TILES_PER_BLOCK, CLASSES], F32, tag="rt", name="rt")
            for jl in range(TILES_PER_BLOCK):
                nc.tensor.transpose(rsum_t[i][:, jl, :], esum[i][:, jl * P : (jl + 1) * P], identity[:])

        def times_gamma(i):
            ratio[i] = two.tile([P, TILES_PER_BLOCK, CLASSES], F32, name="rr")
            js = slice(i * TILES_PER_BLOCK, (i + 1) * TILES_PER_BLOCK)
            nc.vector.tensor_tensor(out=ratio[i][:], in0=rsum_t[i][:], in1=gamma_sb[:, js, :], op=ALU.mult)
            result[i] = outp.tile([P, TILES_PER_BLOCK, CLASSES * MODES], F32, name="o_sb")

        def transpose_expo(i, jl):
            drained = TILES_PER_BLOCK * i + jl - FIRST_DRAIN_TILE
            bank = DRAIN_BANKS[drained % len(DRAIN_BANKS)] if drained >= 0 else "et%d" % (jl % 2)
            expo_t[(i, jl)] = psum.tile([P, MODES, CLASSES], F32, tag=bank, name="et")
            for m in range(MODES):
                nc.tensor.transpose(expo_t[(i, jl)][:, m, :], expo[i][:, m, jl * P : (jl + 1) * P], identity[:])

        def finish_tile(i, jl):
            nc.vector.tensor_tensor(
                out=result[i][:, jl, :].rearrange("p (k m) -> p k m", m=MODES),
                in0=expo_t[(i, jl)][:].rearrange("p m k -> p k m"),
                in1=ratio[i][:, jl, :].unsqueeze(2).to_broadcast([P, CLASSES, MODES]),
                op=ALU.mult,
            )
            nc.sync.dma_start(out=out_rows[:, i * TILES_PER_BLOCK + jl, :], in_=result[i][:, jl, :])

        with tc.tile_pool(name="prep", bufs=1) as prep:
            var_sb = prep.tile([P, MODES, FEATURES], BF16, name="var_sb")
            mu_sb = prep.tile([P, MODES, FEATURES], BF16, name="mu_sb")
            pi_sb = prep.tile([P, MODES], BF16, name="pi_sb")
            nc.scalar.dma_start(out=pi_sb[:], in_=pi)
            for m in range(MODES):
                nc.sync.dma_start(out=var_sb[:, m, :], in_=cur_var[:, m, :])
            load_x(0)
            nc.sync.dma_start(out=mu_sb[:], in_=mu)
            for i in range(1, AHEAD + 1):
                load_x(i)
            make_identity(nc, identity[:])

            ln_var = prep.tile([P, MODES, FEATURES], F32, name="lnv")
            seed = prep.tile([P, MODES, PACK, P], F32, name="y0p")
            neg_iv = prep.tile([P, MODES, PACK, P], F32, name="nivp")
            neg_mu_iv = prep.tile([P, MODES, PACK, P], F32, name="nmivp")
            neg_mu2_iv = prep.tile([P, MODES, PACK, P], F32, name="tmp")
            w_grouped = prep.tile([P, 2, MODES, CLASSES * PACK], BF16, name="wg", align_bytes=64)
            log_det = prep.tile([P, MODES], F32, name="ld")
            pi_eps = prep.tile([P, MODES], F32, name="pif")
            ln_pi = prep.tile([P, MODES], F32, name="lnpi")
            neg_quad = prep.tile([P, MODES], F32, name="qs")
            bias = prep.tile([P, MODES], F32, name="bias")
            w_t = {}

            def by_value(ap):
                return ap.rearrange("k (u q e) -> k u e q", u=2, e=2)

            def split(ap):
                return ap.rearrange("k (u e) q -> k u e q", e=2)

            def flat(ap):
                return ap.rearrange("k t q -> k (t q)")

            nc.gpsimd.tensor_scalar(out=pi_eps[:], in0=pi_sb[:], scalar1=1e-10, scalar2=0.0, op0=ALU.add, op1=ALU.add)
            for m in range(MODES):
                nc.scalar.activation(
                    out=ln_var[:, m, :], in_=var_sb[:, m, :], func=ACT.Ln, accum_out=log_det[:, m : m + 1]
                )
            nc.scalar.activation(out=ln_pi[:], in_=pi_eps[:], func=ACT.Ln)

            for h in range(2):
                transpose_x(0, h)
            for h in range(2):
                copy_x(0, h, True)
            quantise_x(0)

            for m in range(MODES):
                nc.scalar.activation(out=split(seed[:, m, :, :]), in_=by_value(ln_var[:, m, :]), func=ACT.Exp, scale=-1.0)
            for h in range(2):
                square_x(0, h)
            for h in range(2):
                transpose_x(1, h)

            for m in range(MODES):
                nc.vector.tensor_tensor(
                    out=split(neg_iv[:, m, :, :]), in0=by_value(var_sb[:, m, :]), in1=split(seed[:, m, :, :]), op=ALU.mult
                )
                nc.vector.scalar_tensor_tensor(
                    out=flat(neg_iv[:, m, :, :]),
                    in0=flat(neg_iv[:, m, :, :]),
                    scalar=2.0,
                    in1=flat(seed[:, m, :, :]),
                    op0=ALU.subtract,
                    op1=ALU.mult,
                )
                nc.vector.tensor_tensor(
                    out=split(neg_mu_iv[:, m, :, :]), in0=by_value(mu_sb[:, m, :]), in1=split(neg_iv[:, m, :, :]), op=ALU.mult
                )
                nc.gpsimd.tensor_tensor(
                    out=split(neg_mu2_iv[:, m, :, :]),
                    in0=by_value(mu_sb[:, m, :]),
                    in1=split(neg_mu_iv[:, m, :, :]),
                    op=ALU.mult,
                )
                sign = -1.0 if m == 0 else 1.0
                for w, src in enumerate((neg_iv, neg_mu_iv)):
                    w_t[w] = psum.tile(
                        [P, PACK, CLASSES], F32, tag=WEIGHT_BANKS[(2 * m + w) % len(WEIGHT_BANKS)], name="wt"
                    )
                    for t in range(PACK):
                        nc.tensor.transpose(w_t[w][:, t, :], src[:, m, t, :], identity[:])
                for w, factor in enumerate((0.5 * sign, -1.0 * sign)):
                    nc.scalar.activation(
                        out=w_grouped[:, w, m, :].rearrange("p (k t) -> p k t", t=PACK),
                        in_=w_t[w][:].rearrange("p t k -> p k t"),
                        func=ACT.Copy,
                        scale=factor,
                    )
                nc.scalar.activation(
                    out=flat(neg_mu2_iv[:, m, :, :]),
                    in_=flat(neg_mu2_iv[:, m, :, :]),
                    func=ACT.Copy,
                    accum_out=neg_quad[:, m : m + 1],
                )

            quantise_xx(0)
            for m in range(MODES):
                for w in range(2):
                    nc.vector.quantize_mx(
                        out=w_words[:, w, m, :].bitcast(FP8X4), scales=w_scales[:, w, m, :], in_=w_grouped[:, w, m, :]
                    )
                if m >= 1:
                    mx_group(0, m)

            nc.vector.tensor_tensor(out=neg_quad[:], in0=neg_quad[:], in1=log_det[:], op=ALU.subtract)
            nc.vector.scalar_tensor_tensor(
                out=bias[:], in0=neg_quad[:], scalar=0.5, in1=ln_pi[:], op0=ALU.mult, op1=ALU.add
            )
            nc.vector.tensor_scalar(out=dbias[:], in0=bias[:], scalar1=bias[:, 0:1], scalar2=None, op0=ALU.subtract)

            copy_and_square_x(1)
            for h in range(2):
                transpose_x(2, h)
            copy_and_square_x(2)

        big = ctx.enter_context(tc.tile_pool(name="big", bufs=LAG + 1))

        for t in range(BLOCKS + LAG):
            done = t - LAG
            if is_block(t + AHEAD + 1):
                load_x(t + AHEAD + 1)
            if t < GAMMA_LOADS:
                load_gamma(t)
            if is_block(t - 1):
                exponentials(t - 1)
                sum_modes(t - 1)
            for n in range(2):
                if is_block(t):
                    running_max(t, n + 1)
                if is_block(done):
                    finish_tile(done, n)
            if is_block(t):
                running_max(t, 3)
            for n in range(2):
                if is_block(done):
                    transpose_expo(done, n + 2)
                if is_block(t + AHEAD):
                    transpose_x(t + AHEAD, n)
            if is_block(done + 1):
                transpose_rsum(done + 1)
            for n in range(2):
                if is_block(t):
                    subtract_max(t, n + 1)
                if is_block(done):
                    finish_tile(done, n + 2)
            if is_block(t):
                subtract_max(t, 3)
            if t == 0:
                quantise_x(1)
                quantise_xx(1)
            for n in range(2):
                if is_block(t + 1):
                    mx_group(t + 1, n + 1)
                if is_block(done + 1):
                    transpose_expo(done + 1, n)
            if is_block(t + 1):
                mx_group(t + 1, 3)
            if is_block(t + 2):
                quantise_x(t + 2)
                quantise_xx(t + 2)
            if is_block(done + 1):
                times_gamma(done + 1)
            if is_block(t + AHEAD):
                copy_and_square_x(t + AHEAD)
            first = t - LN_DELAY - (GROUP - 1)
            if is_block(first) and first % GROUP == 0:
                reciprocal_sums(first)
